import numpy as np
import ml_dtypes


def mxq(x, axis, fmt="e4m3"):
    dtype, down = {"e4m3": (ml_dtypes.float8_e4m3fn, 7), "e5m2": (ml_dtypes.float8_e5m2, 14)}[fmt]
    v = np.moveaxis(np.asarray(x, np.float32).astype(ml_dtypes.bfloat16).astype(np.float64), axis, -1)
    blocks = v.reshape(v.shape[:-1] + (-1, 32))
    amax = np.abs(blocks).max(-1, keepdims=True)
    byte = np.maximum(np.where(amax > 0, np.frexp(amax)[1] - 1 + 127, 0) - down, 1)
    scale = np.exp2(byte - 127.0)
    codes = (blocks / scale).astype(np.float32).astype(dtype).astype(np.float64)
    return np.moveaxis((codes * scale).reshape(v.shape), -1, axis)


WIDE = False


def mx_kscale(k):
    if not WIDE:
        return np.ones(k)
    levels = np.array([10, -10, 5, -5, 0])
    a = np.random.permutation(np.resize(levels, k // 512 * 4)).reshape(k // 512, 4)
    idx = np.arange(k)
    return np.exp2(a[idx // 512, idx % 128 // 32])


BF16 = ml_dtypes.bfloat16


def bf(x):
    return np.asarray(x, np.float32).astype(BF16)


def f64(x):
    return np.asarray(x).astype(np.float64)


B, S, D, H, DK, DV, C = 1, 1024, 1024, 16, 128, 128, 512
EPS = 1e-5


def silu(a):
    return a / (1.0 + np.exp(-a))


def setup_inputs():
    s = mx_kscale(D)
    ret = np.random.standard_normal((B, H, S, DV)) + 0.3 * np.random.standard_normal((B, H, S, 1))
    return {"x": bf(np.random.standard_normal((B, S, D)) * s),
            "ret": bf(ret * 0.018 * np.sqrt(DK * S)),
            "Wg": bf(np.random.standard_normal((D, H * DV)) / np.sqrt(D) / s[:, None]),
            "bg": bf(np.random.standard_normal(H * DV) * 0.2),
            "Wo": bf(np.random.standard_normal((H * DV, D)) / np.sqrt(H * DV)),
            "bo": bf(np.random.standard_normal(D) * 0.1)}


def reference(x, ret, Wg, bg, Wo, bo):
    concat = f64(ret).transpose(0, 2, 1, 3).reshape(B * S, H, DV)
    mu = concat.mean(-1, keepdims=True)
    var = ((concat - mu) ** 2).mean(-1, keepdims=True)
    gn = ((concat - mu) / np.sqrt(var + EPS)).reshape(B, S, H * DV)
    gate = silu((mxq(f64(x), 2, "e4m3") @ mxq(f64(Wg), 0, "e4m3")) + f64(bg))
    h = gate * gn
    return (mxq(h, 2, "e4m3") @ mxq(f64(Wo), 0, "e4m3")) + f64(bo)

@@ -1,0 +1,342 @@
+from contextlib import ExitStack
+
+import concourse.mybir as mybir
+from concourse.masks import make_identity
+
+F32 = mybir.dt.float32
+BF16 = mybir.dt.bfloat16
+U32 = mybir.dt.uint32
+U8 = mybir.dt.uint8
+FP8X4 = mybir.dt.float8_e4m3fn_x4
+ALU = mybir.AluOpType
+ACT = mybir.ActivationFunctionType
+
+P = 128
+PACK = 4
+S = 1024
+D = 1024
+HEADS = 16
+DV = 128
+F = HEADS * DV
+EPS = 1e-5
+
+TILES = S // P
+QUARTERS = 4
+QCOLS = S // QUARTERS
+QTILES = TILES // QUARTERS
+PASSES1 = D // (P * PACK)
+PASSES2 = F // (P * PACK)
+WG_CHUNKS = 4
+WG_COLS = F // WG_CHUNKS
+N_HALF = 512
+
+FLOPS = 2 * S * D * F + 2 * S * F * D
+
+
+def regroup_views(dst, src):
+    return (
+        dst.rearrange("p (c i) t -> p c t i", i=4),
+        src.rearrange("p t (c i) -> p c t i", i=4),
+    )
+
+
+def tile_gatedmultiscaleretentionlayer_pc_kernel(tc, x, ret, Wg, bg, Wo, bo, out):
+    nc = tc.nc
+
+    x_rows = x.flatten_outer_dims().rearrange("(p i) d -> p i d", i=TILES)
+    ret_rows = ret.rearrange("b h (p i) v -> p (b h) i v", i=TILES)
+    wg_rows = Wg.rearrange("(a p e) f -> p a e f", a=2 * PASSES1, p=P, e=2)
+    wo_rows = Wo.rearrange("(g t p) n -> p g t n", g=PASSES2, t=PACK, p=P)
+    out_rows = out.flatten_outer_dims().rearrange("(p i) n -> p i n", i=TILES)
+
+    with ExitStack() as pools:
+        const = pools.enter_context(tc.tile_pool(name="const", bufs=1))
+        codes = pools.enter_context(tc.tile_pool(name="codes", bufs=1))
+        x_pool = pools.enter_context(tc.tile_pool(name="x_pool", bufs=2))
+        ret_pool = pools.enter_context(tc.tile_pool(name="ret_pool", bufs=4))
+        raw_pool = pools.enter_context(tc.tile_pool(name="raw_pool", bufs=3))
+        grp_pool = pools.enter_context(tc.tile_pool(name="grp_pool", bufs=2))
+        stat_pool = pools.enter_context(tc.tile_pool(name="stat_pool", bufs=2))
+        gn_pool = pools.enter_context(tc.tile_pool(name="gn_pool", bufs=3))
+        gate_pool = pools.enter_context(tc.tile_pool(name="gate_pool", bufs=2))
+        h_pool = pools.enter_context(tc.tile_pool(name="h_pool", bufs=2))
+        out_pool = pools.enter_context(tc.tile_pool(name="out_pool", bufs=2))
+        ps_gate = pools.enter_context(tc.psum_pool(name="ps_gate", bufs=3))
+        ps_turn = pools.enter_context(tc.psum_pool(name="ps_turn", bufs=3))
+        ps_out = pools.enter_context(tc.psum_pool(name="ps_out", bufs=2))
+
+        x_codes = codes.tile([P, QUARTERS * PASSES1 * QCOLS], U32, align_bytes=64)
+        x_scales = codes.tile([P, QUARTERS * PASSES1 * QCOLS], U8, align_bytes=64)
+        wg_codes = codes.tile([P, WG_CHUNKS * PASSES1 * WG_COLS], U32, align_bytes=64)
+        wg_scales = codes.tile([P, WG_CHUNKS * PASSES1 * WG_COLS], U8, align_bytes=64)
+        wo_codes = codes.tile([P, PASSES2 * D], U32, align_bytes=64)
+        wo_scales = codes.tile([P, PASSES2 * D], U8, align_bytes=64)
+
+        ident_f32 = const.tile([P, P], F32)
+        make_identity(nc, ident_f32[:])
+        ident_bf16 = const.tile([P, P], BF16)
+        make_identity(nc, ident_bf16[:])
+        neg_half = const.tile([P, HEADS * QTILES], F32)
+        nc.vector.memset(neg_half[:], -0.5)
+        bg_rows = const.tile([P, P], BF16)
+        bg_cols = const.tile([P, HEADS], F32)
+        bo_all = const.tile([P, D], BF16)
+
+        x_tiles = {}
+        ret_tiles = {}
+        raw_tiles = {}
+        norm_scalars = {}
+        gn_tiles = {}
+        gate_tiles = {}
+        h_tiles = {}
+
+        def load_x(q):
+            x_q = x_pool.tile([P, QTILES, D], BF16, name="x_q")
+            nc.sync.dma_start(out=x_q[:], in_=x_rows[:, q * QTILES : (q + 1) * QTILES, :])
+            x_tiles[q] = x_q
+
+        def load_ret(q):
+            ret_q = ret_pool.tile([P, HEADS, QTILES, DV], BF16, name="ret_q")
+            nc.sync.dma_start(out=ret_q[:], in_=ret_rows[:, :, q * QTILES : (q + 1) * QTILES, :])
+            ret_tiles[q] = ret_q
+
+        def load_wg(c):
+            wg_raw = raw_pool.tile([P, PASSES1 * PACK, WG_COLS], BF16, name="wg_raw", tag="raw")
+            by_e = wg_raw[:].rearrange("p (a e) f -> p a e f", e=2)
+            for e in range(2):
+                nc.sync.dma_start(
+                    out=by_e[:, :, e, :], in_=wg_rows[:, :, e, c * WG_COLS : (c + 1) * WG_COLS]
+                )
+            raw_tiles["wg", c] = wg_raw
+
+        def load_wo(g):
+            wo_raw = raw_pool.tile([P, PACK, D], BF16, name="wo_raw", tag="raw")
+            nc.sync.dma_start(out=wo_raw[:], in_=wo_rows[:, g, :, :])
+            raw_tiles["wo", g] = wo_raw
+
+        def prepare_biases():
+            nc.vector.memset(bg_rows[:], 0.0)
+            nc.scalar.dma_start(out=bg_rows[0:HEADS, :], in_=bg.rearrange("(j p) -> j p", p=P))
+            bg_turned = ps_turn.tile([P, P], BF16, name="bg_turned", tag="turn")
+            nc.tensor.transpose(out=bg_turned[:], in_=bg_rows[:], identity=ident_bf16[:])
+            nc.vector.tensor_copy(out=bg_cols[:], in_=bg_turned[:, 0:HEADS])
+
+        def load_bo():
+            nc.sync.dma_start(out=bo_all[:], in_=bo.partition_broadcast(P))
+
+        def prepare_x(q):
+            x_q = x_tiles[q]
+            x_grouped = grp_pool.tile([P, PASSES1 * QCOLS * PACK], BF16, name="x_grouped", align_bytes=64)
+            grouped_words = x_grouped[:].bitcast(F32).rearrange(
+                "w (g c u) -> w g c u", g=PASSES1, c=QCOLS, u=2
+            )
+            for a in range(QTILES):
+                words = x_q[:, a, :].bitcast(F32)
+                turned = ps_turn.tile([P, PASSES1, 2, P], F32, name="x_turned", tag="turn")
+                for g in range(PASSES1):
+                    for u in range(2):
+                        first = 256 * g + 128 * u
+                        nc.tensor.transpose(
+                            out=turned[:, g, u, :], in_=words[:, first : first + P], identity=ident_f32[:]
+                        )
+                nc.scalar.copy(
+                    out=grouped_words[:, :, a * P : (a + 1) * P, :],
+                    in_=turned[:].rearrange("w g u p -> w g p u"),
+                )
+            cols = slice(q * PASSES1 * QCOLS, (q + 1) * PASSES1 * QCOLS)
+            nc.vector.quantize_mx(
+                out=x_codes[:, cols].bitcast(FP8X4), scales=x_scales[:, cols], in_=x_grouped[:]
+            )
+
+        def prepare_wg(c):
+            wg_raw = raw_tiles["wg", c]
+            wg_grouped = grp_pool.tile([P, PASSES1 * WG_COLS * PACK], BF16, name="wg_grouped", tag="w_grouped", align_bytes=64)
+            grouped = wg_grouped[:].rearrange("p (g f t) -> p g f t", g=PASSES1, f=WG_COLS, t=PACK)
+            dst, src = regroup_views(grouped[:, 0, :, :], wg_raw[:, 0:PACK, :])
+            nc.scalar.copy(out=dst, in_=src)
+            for half in range(2):
+                f_cols = slice(half * WG_COLS // 2, (half + 1) * WG_COLS // 2)
+                dst, src = regroup_views(grouped[:, 1, f_cols, :], wg_raw[:, PACK : 2 * PACK, f_cols])
+                nc.gpsimd.tensor_scalar(out=dst, in0=src, scalar1=1.0, scalar2=0.0, op0=ALU.mult, op1=ALU.add)
+            cols = slice(c * PASSES1 * WG_COLS, (c + 1) * PASSES1 * WG_COLS)
+            nc.vector.quantize_mx(
+                out=wg_codes[:, cols].bitcast(FP8X4), scales=wg_scales[:, cols], in_=wg_grouped[:]
+            )
+
+        def prepare_wo(g):
+            wo_raw = raw_tiles["wo", g]
+            wo_grouped = grp_pool.tile([P, D * PACK], BF16, name="wo_grouped", tag="w_grouped", align_bytes=64)
+            grouped = wo_grouped[:].rearrange("p (n t) -> p n t", t=PACK)
+            for piece in range(4):
+                n_cols = slice(piece * D // 4, (piece + 1) * D // 4)
+                dst, src = regroup_views(grouped[:, n_cols, :], wo_raw[:, :, n_cols])
+                nc.gpsimd.tensor_scalar(out=dst, in0=src, scalar1=1.0, scalar2=0.0, op0=ALU.mult, op1=ALU.add)
+            cols = slice(g * D, (g + 1) * D)
+            nc.vector.quantize_mx(
+                out=wo_codes[:, cols].bitcast(FP8X4), scales=wo_scales[:, cols], in_=wo_grouped[:]
+            )
+
+        def norm_statistics(q):
+            ret_q = ret_tiles[q]
+            groups = HEADS * QTILES
+            stats = stat_pool.tile([P, HEADS, QTILES, 6], F32, name="stats")
+            for h in range(HEADS):
+                for a in range(QTILES):
+                    nc.vector.bn_stats(out=stats[:, h, a, :], in_=ret_q[:, h, a, :])
+            by_group = stats[:].rearrange("p h a k -> p (h a) k")
+            mean_e, cv_e = by_group[:, :, 1], by_group[:, :, 2]
+            mean_o, cv_o = by_group[:, :, 4], by_group[:, :, 5]
+            diff = stat_pool.tile([P, groups], F32, name="diff")
+            nc.vector.tensor_tensor(out=diff[:], in0=mean_e, in1=mean_o, op=ALU.subtract)
+            mean2 = stat_pool.tile([P, groups], F32, name="mean2")
+            nc.vector.tensor_tensor(out=mean2[:], in0=mean_e, in1=mean_o, op=ALU.add)
+            diff_sq = stat_pool.tile([P, groups], F32, name="diff_sq")
+            nc.vector.tensor_tensor(out=diff_sq[:], in0=diff[:], in1=diff[:], op=ALU.mult)
+            cv = stat_pool.tile([P, groups], F32, name="cv")
+            nc.vector.tensor_tensor(out=cv[:], in0=cv_e, in1=cv_o, op=ALU.add)
+            nc.vector.scalar_tensor_tensor(
+                out=cv[:], in0=diff_sq[:], scalar=float(DV // 4), in1=cv[:], op0=ALU.mult, op1=ALU.add
+            )
+            var_eps = stat_pool.tile([P, groups], F32, name="var_eps")
+            nc.vector.tensor_scalar(
+                out=var_eps[:], in0=cv[:], scalar1=1.0 / DV, scalar2=EPS, op0=ALU.mult, op1=ALU.add
+            )
+            rstd = stat_pool.tile([P, groups], F32, name="rstd")
+            nc.gpsimd.tensor_tensor(out=rstd[:], in0=var_eps[:], in1=neg_half[:], op=ALU.pow)
+            shift = stat_pool.tile([P, groups], F32, name="shift")
+            nc.vector.scalar_tensor_tensor(
+                out=shift[:], in0=mean2[:], scalar=-0.5, in1=rstd[:], op0=ALU.mult, op1=ALU.mult
+            )
+            norm_scalars[q] = (rstd, shift)
+
+        def normalise(i):
+            q, a = divmod(i, QTILES)
+            ret_q = ret_tiles[q]
+            rstd, shift = norm_scalars[q]
+            gn = gn_pool.tile([P, HEADS, DV], F32, name="gn")
+            for h in range(HEADS):
+                group = h * QTILES + a
+                nc.scalar.activation(
+                    out=gn[:, h, :],
+                    in_=ret_q[:, h, a, :],
+                    func=ACT.Identity,
+                    scale=rstd[:, group : group + 1],
+                    bias=shift[:, group : group + 1],
+                )
+            gn_tiles[i] = gn
+
+        def gate_quarter(q):
+            gate = gate_pool.tile([P, HEADS, QCOLS], F32, name="gate")
+            for pair in range(HEADS // 2):
+                bank = ps_gate.tile([P, 2, QCOLS], F32, name="gate_bank")
+                for k in range(2):
+                    c, r = divmod(2 * pair + k, WG_COLS // P)
+                    for g in range(PASSES1):
+                        w_cols = slice((c * PASSES1 + g) * WG_COLS + r * P, (c * PASSES1 + g) * WG_COLS + (r + 1) * P)
+                        x_cols = slice((q * PASSES1 + g) * QCOLS, (q * PASSES1 + g + 1) * QCOLS)
+                        nc.tensor.matmul_mx(
+                            out=bank[:, k, :],
+                            lhsT=wg_codes[:, w_cols].bitcast(FP8X4),
+                            lhsT_scale=wg_scales[:, w_cols],
+                            rhs=x_codes[:, x_cols].bitcast(FP8X4),
+                            rhs_scale=x_scales[:, x_cols],
+                            start=(g == 0),
+                            stop=(g == PASSES1 - 1),
+                        )
+                for k in range(2):
+                    head = 2 * pair + k
+                    nc.scalar.activation(
+                        out=gate[:, head, :],
+                        in_=bank[:, k, :],
+                        func=ACT.Silu,
+                        bias=bg_cols[:, head : head + 1],
+                        scale=1.0,
+                    )
+            gate_tiles[q] = gate
+
+        def h_tile(i):
+            q, a = divmod(i, QTILES)
+            gate = gate_tiles[q]
+            gn = gn_tiles[i]
+            h_grouped = h_pool.tile([P, PASSES2 * P * PACK], BF16, name="h_grouped", align_bytes=64)
+            grouped = h_grouped[:].rearrange("v (g p t) -> v g p t", g=PASSES2, p=P, t=PACK)
+            for g in range(PASSES2):
+                turned = ps_turn.tile([P, PACK, P], F32, name="gn_turned", tag="turn")
+                for t in range(PACK):
+                    nc.tensor.transpose(out=turned[:, t, :], in_=gn[:, PACK * g + t, :], identity=ident_f32[:])
+                nc.vector.tensor_tensor(
+                    out=grouped[:, g, :, :],
+                    in0=gate[:, PACK * g : PACK * (g + 1), a * P : (a + 1) * P].rearrange("v t p -> v p t"),
+                    in1=turned[:].rearrange("v t p -> v p t"),
+                    op=ALU.mult,
+                )
+            h_codes = h_pool.tile([P, PASSES2 * P], U32, name="h_codes", align_bytes=64)
+            h_scales = h_pool.tile([P, PASSES2 * P], U8, name="h_scales", align_bytes=64)
+            nc.vector.quantize_mx(out=h_codes[:].bitcast(FP8X4), scales=h_scales[:], in_=h_grouped[:])
+            h_tiles[i] = (h_codes, h_scales)
+
+        def out_tile(i):
+            h_codes, h_scales = h_tiles[i]
+            result = out_pool.tile([P, D], F32, name="result")
+            for half in range(D // N_HALF):
+                acc = ps_out.tile([P, N_HALF], F32, name="acc")
+                for g in range(PASSES2):
+                    h_cols = slice(g * P, (g + 1) * P)
+                    n_cols = slice(g * D + half * N_HALF, g * D + (half + 1) * N_HALF)
+                    nc.tensor.matmul_mx(
+                        out=acc[:],
+                        lhsT=h_codes[:, h_cols].bitcast(FP8X4),
+                        lhsT_scale=h_scales[:, h_cols],
+                        rhs=wo_codes[:, n_cols].bitcast(FP8X4),
+                        rhs_scale=wo_scales[:, n_cols],
+                        start=(g == 0),
+                        stop=(g == PASSES2 - 1),
+                    )
+                n_out = slice(half * N_HALF, (half + 1) * N_HALF)
+                nc.vector.tensor_tensor(out=result[:, n_out], in0=acc[:], in1=bo_all[:, n_out], op=ALU.add)
+            nc.sync.dma_start(out=out_rows[:, i, :], in_=result[:])
+
+        load_ret(0)
+        load_x(0)
+        load_wg(0)
+        load_wg(1)
+        load_ret(1)
+        load_wg(2)
+        prepare_biases()
+        prepare_x(0)
+        norm_statistics(0)
+        prepare_wg(0)
+        load_wg(3)
+        load_x(1)
+        prepare_wg(1)
+        load_wo(0)
+        prepare_wg(2)
+        load_wo(1)
+        prepare_wg(3)
+        load_wo(2)
+        normalise(0)
+        normalise(1)
+        gate_quarter(0)
+        prepare_x(1)
+        norm_statistics(1)
+        prepare_wo(0)
+        load_wo(3)
+        load_ret(2)
+        load_x(2)
+        prepare_wo(1)
+        prepare_wo(2)
+        prepare_wo(3)
+        load_x(3)
+        load_ret(3)
+        load_bo()
+        for q in range(QUARTERS):
+            if q + 1 < QUARTERS:
+                gate_quarter(q + 1)
+            if q + 2 < QUARTERS:
+                prepare_x(q + 2)
+                norm_statistics(q + 2)
+            for i in range(q * QTILES, (q + 1) * QTILES):
+                h_tile(i)
+                out_tile(i)
+                if i + QTILES < TILES:
+                    normalise(i + QTILES)

@@ -40,6 +40,10 @@ def regroup_views(dst, src):
     )
 
 
+def regroup_views_one_hop(dst, src):
+    return dst, src.rearrange("p t c -> p c t")
+
+
 def tile_gatedmultiscaleretentionlayer_pc_kernel(tc, x, ret, Wg, bg, Wo, bo, out):
     nc = tc.nc
 
@@ -156,7 +160,7 @@ def tile_gatedmultiscaleretentionlayer_pc_kernel(tc, x, ret, Wg, bg, Wo, bo, out
             nc.scalar.copy(out=dst, in_=src)
             for half in range(2):
                 f_cols = slice(half * WG_COLS // 2, (half + 1) * WG_COLS // 2)
-                dst, src = regroup_views(grouped[:, 1, f_cols, :], wg_raw[:, PACK : 2 * PACK, f_cols])
+                dst, src = regroup_views_one_hop(grouped[:, 1, f_cols, :], wg_raw[:, PACK : 2 * PACK, f_cols])
                 nc.gpsimd.tensor_scalar(out=dst, in0=src, scalar1=1.0, scalar2=0.0, op0=ALU.mult, op1=ALU.add)
             cols = slice(c * PASSES1 * WG_COLS, (c + 1) * PASSES1 * WG_COLS)
             nc.vector.quantize_mx(
@@ -169,7 +173,7 @@ def tile_gatedmultiscaleretentionlayer_pc_kernel(tc, x, ret, Wg, bg, Wo, bo, out
             grouped = wo_grouped[:].rearrange("p (n t) -> p n t", t=PACK)
             for piece in range(4):
                 n_cols = slice(piece * D // 4, (piece + 1) * D // 4)
-                dst, src = regroup_views(grouped[:, n_cols, :], wo_raw[:, :, n_cols])
+                dst, src = regroup_views_one_hop(grouped[:, n_cols, :], wo_raw[:, :, n_cols])
                 nc.gpsimd.tensor_scalar(out=dst, in0=src, scalar1=1.0, scalar2=0.0, op0=ALU.mult, op1=ALU.add)
             cols = slice(g * D, (g + 1) * D)
             nc.vector.quantize_mx(

@@ -29,6 +29,7 @@ PASSES2 = F // (P * PACK)
 WG_CHUNKS = 4
 WG_COLS = F // WG_CHUNKS
 N_HALF = 512
+OUT_LAG = 2
 
 FLOPS = 2 * S * D * F + 2 * S * F * D
 
@@ -38,10 +39,6 @@ def regroup_views(dst, src):
         dst.rearrange("p (c i) t -> p c t i", i=4),
         src.rearrange("p t (c i) -> p c t i", i=4),
     )
-
-
-def regroup_views_one_hop(dst, src):
-    return dst, src.rearrange("p t c -> p c t")
 
 
 def tile_gatedmultiscaleretentionlayer_pc_kernel(tc, x, ret, Wg, bg, Wo, bo, out):
@@ -58,41 +55,42 @@ def tile_gatedmultiscaleretentionlayer_pc_kernel(tc, x, ret, Wg, bg, Wo, bo, out
         codes = pools.enter_context(tc.tile_pool(name="codes", bufs=1))
         x_pool = pools.enter_context(tc.tile_pool(name="x_pool", bufs=2))
         ret_pool = pools.enter_context(tc.tile_pool(name="ret_pool", bufs=4))
-        raw_pool = pools.enter_context(tc.tile_pool(name="raw_pool", bufs=3))
+        raw_pool = pools.enter_context(tc.tile_pool(name="raw_pool", bufs=4))
         grp_pool = pools.enter_context(tc.tile_pool(name="grp_pool", bufs=2))
         stat_pool = pools.enter_context(tc.tile_pool(name="stat_pool", bufs=2))
         gn_pool = pools.enter_context(tc.tile_pool(name="gn_pool", bufs=3))
         gate_pool = pools.enter_context(tc.tile_pool(name="gate_pool", bufs=2))
         h_pool = pools.enter_context(tc.tile_pool(name="h_pool", bufs=2))
+        hc_pool = pools.enter_context(tc.tile_pool(name="hc_pool", bufs=OUT_LAG + 2))
         out_pool = pools.enter_context(tc.tile_pool(name="out_pool", bufs=2))
         ps_gate = pools.enter_context(tc.psum_pool(name="ps_gate", bufs=3))
         ps_turn = pools.enter_context(tc.psum_pool(name="ps_turn", bufs=3))
         ps_out = pools.enter_context(tc.psum_pool(name="ps_out", bufs=2))
+        pools.enter_context(tc.manual_schedule())
 
-        x_codes = codes.tile([P, QUARTERS * PASSES1 * QCOLS], U32, align_bytes=64)
-        x_scales = codes.tile([P, QUARTERS * PASSES1 * QCOLS], U8, align_bytes=64)
-        wg_codes = codes.tile([P, WG_CHUNKS * PASSES1 * WG_COLS], U32, align_bytes=64)
-        wg_scales = codes.tile([P, WG_CHUNKS * PASSES1 * WG_COLS], U8, align_bytes=64)
-        wo_codes = codes.tile([P, PASSES2 * D], U32, align_bytes=64)
-        wo_scales = codes.tile([P, PASSES2 * D], U8, align_bytes=64)
+        x_codes = codes.tile([P, QUARTERS * PASSES1 * QCOLS], U32, name="x_codes", align_bytes=64)
+        x_scales = codes.tile([P, QUARTERS * PASSES1 * QCOLS], U8, name="x_scales", align_bytes=64)
+        wg_codes = codes.tile([P, WG_CHUNKS * PASSES1 * WG_COLS], U32, name="wg_codes", align_bytes=64)
+        wg_scales = codes.tile([P, WG_CHUNKS * PASSES1 * WG_COLS], U8, name="wg_scales", align_bytes=64)
+        wo_codes = codes.tile([P, PASSES2 * D], U32, name="wo_codes", align_bytes=64)
+        wo_scales = codes.tile([P, PASSES2 * D], U8, name="wo_scales", align_bytes=64)
 
-        ident_f32 = const.tile([P, P], F32)
-        make_identity(nc, ident_f32[:])
-        ident_bf16 = const.tile([P, P], BF16)
-        make_identity(nc, ident_bf16[:])
-        neg_half = const.tile([P, HEADS * QTILES], F32)
-        nc.vector.memset(neg_half[:], -0.5)
-        bg_rows = const.tile([P, P], BF16)
-        bg_cols = const.tile([P, HEADS], F32)
-        bo_all = const.tile([P, D], BF16)
+        ident_f32 = const.tile([P, P], F32, name="ident_f32")
+        ident_bf16 = const.tile([P, P], BF16, name="ident_bf16")
+        neg_half = const.tile([P, HEADS * QTILES], F32, name="neg_half")
+        bg_rows = const.tile([P, P], BF16, name="bg_rows")
+        bg_cols = const.tile([P, HEADS], F32, name="bg_cols")
+        bo_all = const.tile([P, D], BF16, name="bo_all")
 
         x_tiles = {}
         ret_tiles = {}
         raw_tiles = {}
+        stat_tiles = {}
         norm_scalars = {}
         gn_tiles = {}
         gate_tiles = {}
         h_tiles = {}
+        hc_tiles = {}
 
         def load_x(q):
             x_q = x_pool.tile([P, QTILES, D], BF16, name="x_q")
@@ -101,7 +99,10 @@ def tile_gatedmultiscaleretentionlayer_pc_kernel(tc, x, ret, Wg, bg, Wo, bo, out
 
         def load_ret(q):
             ret_q = ret_pool.tile([P, HEADS, QTILES, DV], BF16, name="ret_q")
-            nc.sync.dma_start(out=ret_q[:], in_=ret_rows[:, :, q * QTILES : (q + 1) * QTILES, :])
+            for heads in (slice(0, HEADS // 2), slice(HEADS // 2, HEADS)):
+                nc.sync.dma_start(
+                    out=ret_q[:, heads, :, :], in_=ret_rows[:, heads, q * QTILES : (q + 1) * QTILES, :]
+                )
             ret_tiles[q] = ret_q
 
         def load_wg(c):
@@ -118,9 +119,11 @@ def tile_gatedmultiscaleretentionlayer_pc_kernel(tc, x, ret, Wg, bg, Wo, bo, out
             nc.sync.dma_start(out=wo_raw[:], in_=wo_rows[:, g, :, :])
             raw_tiles["wo", g] = wo_raw
 
-        def prepare_biases():
+        def load_bg():
             nc.vector.memset(bg_rows[:], 0.0)
-            nc.scalar.dma_start(out=bg_rows[0:HEADS, :], in_=bg.rearrange("(j p) -> j p", p=P))
+            nc.sync.dma_start(out=bg_rows[0:HEADS, :], in_=bg.rearrange("(j p) -> j p", p=P))
+
+        def turn_bg():
             bg_turned = ps_turn.tile([P, P], BF16, name="bg_turned", tag="turn")
             nc.tensor.transpose(out=bg_turned[:], in_=bg_rows[:], identity=ident_bf16[:])
             nc.vector.tensor_copy(out=bg_cols[:], in_=bg_turned[:, 0:HEADS])
@@ -128,7 +131,7 @@ def tile_gatedmultiscaleretentionlayer_pc_kernel(tc, x, ret, Wg, bg, Wo, bo, out
         def load_bo():
             nc.sync.dma_start(out=bo_all[:], in_=bo.partition_broadcast(P))
 
-        def prepare_x(q):
+        def turn_x(q):
             x_q = x_tiles[q]
             x_grouped = grp_pool.tile([P, PASSES1 * QCOLS * PACK], BF16, name="x_grouped", align_bytes=64)
             grouped_words = x_grouped[:].bitcast(F32).rearrange(
@@ -147,47 +150,56 @@ def tile_gatedmultiscaleretentionlayer_pc_kernel(tc, x, ret, Wg, bg, Wo, bo, out
                     out=grouped_words[:, :, a * P : (a + 1) * P, :],
                     in_=turned[:].rearrange("w g u p -> w g p u"),
                 )
+            x_tiles["grouped", q] = x_grouped
+
+        def quantise_x(q):
             cols = slice(q * PASSES1 * QCOLS, (q + 1) * PASSES1 * QCOLS)
             nc.vector.quantize_mx(
-                out=x_codes[:, cols].bitcast(FP8X4), scales=x_scales[:, cols], in_=x_grouped[:]
+                out=x_codes[:, cols].bitcast(FP8X4), scales=x_scales[:, cols], in_=x_tiles["grouped", q][:]
             )
 
-        def prepare_wg(c):
+        def regroup_wg(c):
             wg_raw = raw_tiles["wg", c]
             wg_grouped = grp_pool.tile([P, PASSES1 * WG_COLS * PACK], BF16, name="wg_grouped", tag="w_grouped", align_bytes=64)
             grouped = wg_grouped[:].rearrange("p (g f t) -> p g f t", g=PASSES1, f=WG_COLS, t=PACK)
             dst, src = regroup_views(grouped[:, 0, :, :], wg_raw[:, 0:PACK, :])
             nc.scalar.copy(out=dst, in_=src)
-            for half in range(2):
-                f_cols = slice(half * WG_COLS // 2, (half + 1) * WG_COLS // 2)
-                dst, src = regroup_views_one_hop(grouped[:, 1, f_cols, :], wg_raw[:, PACK : 2 * PACK, f_cols])
-                nc.gpsimd.tensor_scalar(out=dst, in0=src, scalar1=1.0, scalar2=0.0, op0=ALU.mult, op1=ALU.add)
+            dst, src = regroup_views(grouped[:, 1, :, :], wg_raw[:, PACK : 2 * PACK, :])
+            nc.vector.tensor_copy(out=dst, in_=src)
+            raw_tiles["wg grouped", c] = wg_grouped
+
+        def quantise_wg(c):
             cols = slice(c * PASSES1 * WG_COLS, (c + 1) * PASSES1 * WG_COLS)
             nc.vector.quantize_mx(
-                out=wg_codes[:, cols].bitcast(FP8X4), scales=wg_scales[:, cols], in_=wg_grouped[:]
+                out=wg_codes[:, cols].bitcast(FP8X4), scales=wg_scales[:, cols], in_=raw_tiles["wg grouped", c][:]
             )
 
-        def prepare_wo(g):
+        def regroup_wo(g):
             wo_raw = raw_tiles["wo", g]
             wo_grouped = grp_pool.tile([P, D * PACK], BF16, name="wo_grouped", tag="w_grouped", align_bytes=64)
             grouped = wo_grouped[:].rearrange("p (n t) -> p n t", t=PACK)
-            for piece in range(4):
-                n_cols = slice(piece * D // 4, (piece + 1) * D // 4)
-                dst, src = regroup_views_one_hop(grouped[:, n_cols, :], wo_raw[:, :, n_cols])
-                nc.gpsimd.tensor_scalar(out=dst, in0=src, scalar1=1.0, scalar2=0.0, op0=ALU.mult, op1=ALU.add)
+            dst, src = regroup_views(grouped[:, 0 : D // 2, :], wo_raw[:, :, 0 : D // 2])
+            nc.scalar.copy(out=dst, in_=src)
+            dst, src = regroup_views(grouped[:, D // 2 : D, :], wo_raw[:, :, D // 2 : D])
+            nc.vector.tensor_copy(out=dst, in_=src)
+            raw_tiles["wo grouped", g] = wo_grouped
+
+        def quantise_wo(g):
             cols = slice(g * D, (g + 1) * D)
             nc.vector.quantize_mx(
-                out=wo_codes[:, cols].bitcast(FP8X4), scales=wo_scales[:, cols], in_=wo_grouped[:]
+                out=wo_codes[:, cols].bitcast(FP8X4), scales=wo_scales[:, cols], in_=raw_tiles["wo grouped", g][:]
             )
 
-        def norm_statistics(q):
-            ret_q = ret_tiles[q]
-            groups = HEADS * QTILES
-            stats = stat_pool.tile([P, HEADS, QTILES, 6], F32, name="stats")
+        def tile_statistics(i):
+            q, a = divmod(i, QTILES)
+            if a == 0:
+                stat_tiles[q] = stat_pool.tile([P, HEADS, QTILES, 6], F32, name="stats")
             for h in range(HEADS):
-                for a in range(QTILES):
-                    nc.vector.bn_stats(out=stats[:, h, a, :], in_=ret_q[:, h, a, :])
-            by_group = stats[:].rearrange("p h a k -> p (h a) k")
+                nc.vector.bn_stats(out=stat_tiles[q][:, h, a, :], in_=ret_tiles[q][:, h, a, :])
+
+        def join_statistics(q):
+            groups = HEADS * QTILES
+            by_group = stat_tiles[q][:].rearrange("p h a k -> p (h a) k")
             mean_e, cv_e = by_group[:, :, 1], by_group[:, :, 2]
             mean_o, cv_o = by_group[:, :, 4], by_group[:, :, 5]
             diff = stat_pool.tile([P, groups], F32, name="diff")
@@ -205,12 +217,11 @@ def tile_gatedmultiscaleretentionlayer_pc_kernel(tc, x, ret, Wg, bg, Wo, bo, out
             nc.vector.tensor_scalar(
                 out=var_eps[:], in0=cv[:], scalar1=1.0 / DV, scalar2=EPS, op0=ALU.mult, op1=ALU.add
             )
-            rstd = stat_pool.tile([P, groups], F32, name="rstd")
+            rstd = stat_pool.tile([P, groups], F32, name="rstd", bufs=3)
             nc.gpsimd.tensor_tensor(out=rstd[:], in0=var_eps[:], in1=neg_half[:], op=ALU.pow)
-            shift = stat_pool.tile([P, groups], F32, name="shift")
-            nc.vector.scalar_tensor_tensor(
-                out=shift[:], in0=mean2[:], scalar=-0.5, in1=rstd[:], op0=ALU.mult, op1=ALU.mult
-            )
+            shift = stat_pool.tile([P, groups], F32, name="shift", bufs=3)
+            nc.gpsimd.tensor_tensor(out=shift[:], in0=mean2[:], in1=rstd[:], op=ALU.mult)
+            nc.gpsimd.tensor_scalar(out=shift[:], in0=shift[:], scalar1=-0.5, scalar2=0.0, op0=ALU.mult, op1=ALU.add)
             norm_scalars[q] = (rstd, shift)
 
         def normalise(i):
@@ -229,58 +240,58 @@ def tile_gatedmultiscaleretentionlayer_pc_kernel(tc, x, ret, Wg, bg, Wo, bo, out
                 )
             gn_tiles[i] = gn
 
-        def gate_quarter(q):
-            gate = gate_pool.tile([P, HEADS, QCOLS], F32, name="gate")
-            for pair in range(HEADS // 2):
-                bank = ps_gate.tile([P, 2, QCOLS], F32, name="gate_bank")
-                for k in range(2):
-                    c, r = divmod(2 * pair + k, WG_COLS // P)
-                    for g in range(PASSES1):
-                        w_cols = slice((c * PASSES1 + g) * WG_COLS + r * P, (c * PASSES1 + g) * WG_COLS + (r + 1) * P)
-                        x_cols = slice((q * PASSES1 + g) * QCOLS, (q * PASSES1 + g + 1) * QCOLS)
-                        nc.tensor.matmul_mx(
-                            out=bank[:, k, :],
-                            lhsT=wg_codes[:, w_cols].bitcast(FP8X4),
-                            lhsT_scale=wg_scales[:, w_cols],
-                            rhs=x_codes[:, x_cols].bitcast(FP8X4),
-                            rhs_scale=x_scales[:, x_cols],
-                            start=(g == 0),
-                            stop=(g == PASSES1 - 1),
-                        )
-                for k in range(2):
-                    head = 2 * pair + k
-                    nc.scalar.activation(
-                        out=gate[:, head, :],
-                        in_=bank[:, k, :],
-                        func=ACT.Silu,
-                        bias=bg_cols[:, head : head + 1],
-                        scale=1.0,
-                    )
-            gate_tiles[q] = gate
-
-        def h_tile(i):
-            q, a = divmod(i, QTILES)
+        def gate_pair(q, pair):
+            if pair == 0:
+                gate_tiles[q] = gate_pool.tile([P, HEADS, QCOLS], F32, name="gate")
             gate = gate_tiles[q]
-            gn = gn_tiles[i]
-            h_grouped = h_pool.tile([P, PASSES2 * P * PACK], BF16, name="h_grouped", align_bytes=64)
-            grouped = h_grouped[:].rearrange("v (g p t) -> v g p t", g=PASSES2, p=P, t=PACK)
-            for g in range(PASSES2):
-                turned = ps_turn.tile([P, PACK, P], F32, name="gn_turned", tag="turn")
-                for t in range(PACK):
-                    nc.tensor.transpose(out=turned[:, t, :], in_=gn[:, PACK * g + t, :], identity=ident_f32[:])
-                nc.vector.tensor_tensor(
-                    out=grouped[:, g, :, :],
-                    in0=gate[:, PACK * g : PACK * (g + 1), a * P : (a + 1) * P].rearrange("v t p -> v p t"),
-                    in1=turned[:].rearrange("v t p -> v p t"),
-                    op=ALU.mult,
+            bank = ps_gate.tile([P, 2, QCOLS], F32, name="gate_bank")
+            for k in range(2):
+                c, r = divmod(2 * pair + k, WG_COLS // P)
+                for g in range(PASSES1):
+                    w_cols = slice((c * PASSES1 + g) * WG_COLS + r * P, (c * PASSES1 + g) * WG_COLS + (r + 1) * P)
+                    x_cols = slice((q * PASSES1 + g) * QCOLS, (q * PASSES1 + g + 1) * QCOLS)
+                    nc.tensor.matmul_mx(
+                        out=bank[:, k, :],
+                        lhsT=wg_codes[:, w_cols].bitcast(FP8X4),
+                        lhsT_scale=wg_scales[:, w_cols],
+                        rhs=x_codes[:, x_cols].bitcast(FP8X4),
+                        rhs_scale=x_scales[:, x_cols],
+                        start=(g == 0),
+                        stop=(g == PASSES1 - 1),
+                    )
+            for k in range(2):
+                head = 2 * pair + k
+                nc.scalar.activation(
+                    out=gate[:, head, :],
+                    in_=bank[:, k, :],
+                    func=ACT.Silu,
+                    bias=bg_cols[:, head : head + 1],
+                    scale=1.0,
                 )
-            h_codes = h_pool.tile([P, PASSES2 * P], U32, name="h_codes", align_bytes=64)
-            h_scales = h_pool.tile([P, PASSES2 * P], U8, name="h_scales", align_bytes=64)
-            nc.vector.quantize_mx(out=h_codes[:].bitcast(FP8X4), scales=h_scales[:], in_=h_grouped[:])
-            h_tiles[i] = (h_codes, h_scales)
+
+        def turn_and_multiply(i, g):
+            q, a = divmod(i, QTILES)
+            if g == 0:
+                h_tiles[i] = h_pool.tile([P, PASSES2 * P * PACK], BF16, name="h_grouped", align_bytes=64)
+            grouped = h_tiles[i][:].rearrange("v (g p t) -> v g p t", g=PASSES2, p=P, t=PACK)
+            turned = ps_turn.tile([P, PACK, P], F32, name="gn_turned", tag="turn")
+            for t in range(PACK):
+                nc.tensor.transpose(out=turned[:, t, :], in_=gn_tiles[i][:, PACK * g + t, :], identity=ident_f32[:])
+            nc.vector.tensor_tensor(
+                out=grouped[:, g, :, :],
+                in0=gate_tiles[q][:, PACK * g : PACK * (g + 1), a * P : (a + 1) * P].rearrange("v t p -> v p t"),
+                in1=turned[:].rearrange("v t p -> v p t"),
+                op=ALU.mult,
+            )
+
+        def quantise_h(i):
+            h_codes = hc_pool.tile([P, PASSES2 * P], U32, name="h_codes", align_bytes=64)
+            h_scales = hc_pool.tile([P, PASSES2 * P], U8, name="h_scales", align_bytes=64)
+            nc.vector.quantize_mx(out=h_codes[:].bitcast(FP8X4), scales=h_scales[:], in_=h_tiles[i][:])
+            hc_tiles[i] = (h_codes, h_scales)
 
         def out_tile(i):
-            h_codes, h_scales = h_tiles[i]
+            h_codes, h_scales = hc_tiles[i]
             result = out_pool.tile([P, D], F32, name="result")
             for half in range(D // N_HALF):
                 acc = ps_out.tile([P, N_HALF], F32, name="acc")
@@ -300,47 +311,69 @@ def tile_gatedmultiscaleretentionlayer_pc_kernel(tc, x, ret, Wg, bg, Wo, bo, out
                 nc.vector.tensor_tensor(out=result[:, n_out], in0=acc[:], in1=bo_all[:, n_out], op=ALU.add)
             nc.sync.dma_start(out=out_rows[:, i, :], in_=result[:])
 
+        make_identity(nc, ident_f32[:])
+        make_identity(nc, ident_bf16[:])
+        nc.vector.memset(neg_half[:], -0.5)
+        load_bg()
         load_ret(0)
         load_x(0)
-        load_wg(0)
-        load_wg(1)
+        for c in range(WG_CHUNKS):
+            load_wg(c)
         load_ret(1)
-        load_wg(2)
-        prepare_biases()
-        prepare_x(0)
-        norm_statistics(0)
-        prepare_wg(0)
-        load_wg(3)
         load_x(1)
-        prepare_wg(1)
-        load_wo(0)
-        prepare_wg(2)
-        load_wo(1)
-        prepare_wg(3)
-        load_wo(2)
-        normalise(0)
-        normalise(1)
-        gate_quarter(0)
-        prepare_x(1)
-        norm_statistics(1)
-        prepare_wo(0)
-        load_wo(3)
+
+        tile_statistics(0)
+        tile_statistics(1)
+        join_statistics(0)
+        turn_bg()
+        turn_x(0)
+        quantise_x(0)
+        for c in range(WG_CHUNKS + 1):
+            if c < WG_CHUNKS:
+                regroup_wg(c)
+                load_wo(c)
+            if c >= 1:
+                quantise_wg(c - 1)
+                gate_pair(0, 2 * (c - 1))
+                gate_pair(0, 2 * (c - 1) + 1)
         load_ret(2)
         load_x(2)
-        prepare_wo(1)
-        prepare_wo(2)
-        prepare_wo(3)
-        load_x(3)
         load_ret(3)
         load_bo()
-        for q in range(QUARTERS):
-            if q + 1 < QUARTERS:
-                gate_quarter(q + 1)
-            if q + 2 < QUARTERS:
-                prepare_x(q + 2)
-                norm_statistics(q + 2)
-            for i in range(q * QTILES, (q + 1) * QTILES):
-                h_tile(i)
-                out_tile(i)
+        normalise(0)
+        tile_statistics(2)
+        tile_statistics(3)
+        join_statistics(1)
+        normalise(1)
+        turn_x(1)
+        load_x(3)
+
+        for i in range(TILES + OUT_LAG):
+            q, a = divmod(i, QTILES)
+            if i < TILES:
+                for g in range(PASSES2):
+                    turn_and_multiply(i, g)
+                if a == 0 and q + 2 < QUARTERS:
+                    turn_x(q + 2)
+                quantise_h(i)
+            if i == 0:
+                quantise_x(1)
+            if i < PASSES2 // 2:
+                regroup_wo(2 * i)
+                regroup_wo(2 * i + 1)
+                quantise_wo(2 * i)
+                quantise_wo(2 * i + 1)
+            if i >= OUT_LAG:
+                out_tile(i - OUT_LAG)
+            if i < TILES:
+                if q + 1 < QUARTERS:
+                    for pair in range(4 * a, 4 * a + 4):
+                        gate_pair(q + 1, pair)
                 if i + QTILES < TILES:
                     normalise(i + QTILES)
+                if i + 2 * QTILES < TILES:
+                    tile_statistics(i + 2 * QTILES)
+                    if a == 1:
+                        join_statistics(q + 2)
+                if a == 0 and q + 2 < QUARTERS:
+                    quantise_x(q + 2)

@@ -29,7 +29,8 @@ PASSES2 = F // (P * PACK)
 WG_CHUNKS = 4
 WG_COLS = F // WG_CHUNKS
 N_HALF = 512
-OUT_LAG = 2
+GATE_PAIRS = 6
+OUT_LAG = 1
 
 FLOPS = 2 * S * D * F + 2 * S * F * D
 
@@ -54,12 +55,12 @@ def tile_gatedmultiscaleretentionlayer_pc_kernel(tc, x, ret, Wg, bg, Wo, bo, out
         const = pools.enter_context(tc.tile_pool(name="const", bufs=1))
         codes = pools.enter_context(tc.tile_pool(name="codes", bufs=1))
         x_pool = pools.enter_context(tc.tile_pool(name="x_pool", bufs=2))
-        ret_pool = pools.enter_context(tc.tile_pool(name="ret_pool", bufs=4))
+        ret_pool = pools.enter_context(tc.tile_pool(name="ret_pool", bufs=3))
         raw_pool = pools.enter_context(tc.tile_pool(name="raw_pool", bufs=4))
         grp_pool = pools.enter_context(tc.tile_pool(name="grp_pool", bufs=2))
         stat_pool = pools.enter_context(tc.tile_pool(name="stat_pool", bufs=2))
-        gn_pool = pools.enter_context(tc.tile_pool(name="gn_pool", bufs=3))
-        gate_pool = pools.enter_context(tc.tile_pool(name="gate_pool", bufs=2))
+        gn_pool = pools.enter_context(tc.tile_pool(name="gn_pool", bufs=2))
+        gate_pool = pools.enter_context(tc.tile_pool(name="gate_pool", bufs=3))
         h_pool = pools.enter_context(tc.tile_pool(name="h_pool", bufs=2))
         hc_pool = pools.enter_context(tc.tile_pool(name="hc_pool", bufs=OUT_LAG + 2))
         out_pool = pools.enter_context(tc.tile_pool(name="out_pool", bufs=2))
@@ -179,9 +180,11 @@ def tile_gatedmultiscaleretentionlayer_pc_kernel(tc, x, ret, Wg, bg, Wo, bo, out
             wo_grouped = grp_pool.tile([P, D * PACK], BF16, name="wo_grouped", tag="w_grouped", align_bytes=64)
             grouped = wo_grouped[:].rearrange("p (n t) -> p n t", t=PACK)
             dst, src = regroup_views(grouped[:, 0 : D // 2, :], wo_raw[:, :, 0 : D // 2])
-            nc.scalar.copy(out=dst, in_=src)
-            dst, src = regroup_views(grouped[:, D // 2 : D, :], wo_raw[:, :, D // 2 : D])
             nc.vector.tensor_copy(out=dst, in_=src)
+            nc.gpsimd.tensor_scalar(
+                out=grouped[:, D // 2 : D, :], in0=wo_raw[:, :, D // 2 : D].rearrange("p t n -> p n t"),
+                scalar1=1.0, scalar2=0.0, op0=ALU.mult, op1=ALU.add,
+            )
             raw_tiles["wo grouped", g] = wo_grouped
 
         def quantise_wo(g):
@@ -336,44 +339,43 @@ def tile_gatedmultiscaleretentionlayer_pc_kernel(tc, x, ret, Wg, bg, Wo, bo, out
                 quantise_wg(c - 1)
                 gate_pair(0, 2 * (c - 1))
                 gate_pair(0, 2 * (c - 1) + 1)
-        load_ret(2)
         load_x(2)
-        load_ret(3)
-        load_bo()
+        load_ret(2)
         normalise(0)
-        tile_statistics(2)
-        tile_statistics(3)
-        join_statistics(1)
-        normalise(1)
         turn_x(1)
         load_x(3)
+        normalise(1)
+        load_ret(3)
+        load_bo()
+        tile_statistics(2)
+        tile_statistics(3)
+        for g in range(PASSES2 + 1):
+            if g < PASSES2:
+                regroup_wo(g)
+            if g >= 1:
+                quantise_wo(g - 1)
+        join_statistics(1)
+        quantise_x(1)
 
         for i in range(TILES + OUT_LAG):
             q, a = divmod(i, QTILES)
             if i < TILES:
                 for g in range(PASSES2):
                     turn_and_multiply(i, g)
-                if a == 0 and q + 2 < QUARTERS:
-                    turn_x(q + 2)
+                if i + 2 < QUARTERS:
+                    turn_x(i + 2)
                 quantise_h(i)
-            if i == 0:
-                quantise_x(1)
-            if i < PASSES2 // 2:
-                regroup_wo(2 * i)
-                regroup_wo(2 * i + 1)
-                quantise_wo(2 * i)
-                quantise_wo(2 * i + 1)
             if i >= OUT_LAG:
                 out_tile(i - OUT_LAG)
             if i < TILES:
-                if q + 1 < QUARTERS:
-                    for pair in range(4 * a, 4 * a + 4):
-                        gate_pair(q + 1, pair)
+                for k in range(GATE_PAIRS * i, GATE_PAIRS * (i + 1)):
+                    if k < (QUARTERS - 1) * HEADS // 2:
+                        gate_pair(1 + k // (HEADS // 2), k % (HEADS // 2))
                 if i + QTILES < TILES:
                     normalise(i + QTILES)
                 if i + 2 * QTILES < TILES:
                     tile_statistics(i + 2 * QTILES)
                     if a == 1:
                         join_statistics(q + 2)
-                if a == 0 and q + 2 < QUARTERS:
-                    quantise_x(q + 2)
+                if i + 2 < QUARTERS:
+                    quantise_x(i + 2)

@@ -180,11 +180,9 @@ def tile_gatedmultiscaleretentionlayer_pc_kernel(tc, x, ret, Wg, bg, Wo, bo, out
             wo_grouped = grp_pool.tile([P, D * PACK], BF16, name="wo_grouped", tag="w_grouped", align_bytes=64)
             grouped = wo_grouped[:].rearrange("p (n t) -> p n t", t=PACK)
             dst, src = regroup_views(grouped[:, 0 : D // 2, :], wo_raw[:, :, 0 : D // 2])
+            nc.scalar.copy(out=dst, in_=src)
+            dst, src = regroup_views(grouped[:, D // 2 : D, :], wo_raw[:, :, D // 2 : D])
             nc.vector.tensor_copy(out=dst, in_=src)
-            nc.gpsimd.tensor_scalar(
-                out=grouped[:, D // 2 : D, :], in0=wo_raw[:, :, D // 2 : D].rearrange("p t n -> p n t"),
-                scalar1=1.0, scalar2=0.0, op0=ALU.mult, op1=ALU.add,
-            )
             raw_tiles["wo grouped", g] = wo_grouped
 
         def quantise_wo(g):
@@ -342,19 +340,19 @@ def tile_gatedmultiscaleretentionlayer_pc_kernel(tc, x, ret, Wg, bg, Wo, bo, out
         load_x(2)
         load_ret(2)
         normalise(0)
-        turn_x(1)
-        load_x(3)
-        normalise(1)
-        load_ret(3)
-        load_bo()
         tile_statistics(2)
         tile_statistics(3)
+        join_statistics(1)
         for g in range(PASSES2 + 1):
             if g < PASSES2:
                 regroup_wo(g)
             if g >= 1:
                 quantise_wo(g - 1)
-        join_statistics(1)
+        turn_x(1)
+        load_x(3)
+        normalise(1)
+        load_ret(3)
+        load_bo()
         quantise_x(1)
 
         for i in range(TILES + OUT_LAG):

@@ -31,6 +31,7 @@ WG_COLS = F // WG_CHUNKS
 N_HALF = 512
 GATE_PAIRS = 6
 OUT_LAG = 1
+STAT_LEAD = 4
 
 FLOPS = 2 * S * D * F + 2 * S * F * D
 
@@ -78,7 +79,7 @@ def tile_gatedmultiscaleretentionlayer_pc_kernel(tc, x, ret, Wg, bg, Wo, bo, out
 
         ident_f32 = const.tile([P, P], F32, name="ident_f32")
         ident_bf16 = const.tile([P, P], BF16, name="ident_bf16")
-        neg_half = const.tile([P, HEADS * QTILES], F32, name="neg_half")
+        neg_half = const.tile([P, HEADS], F32, name="neg_half")
         bg_rows = const.tile([P, P], BF16, name="bg_rows")
         bg_cols = const.tile([P, HEADS], F32, name="bg_cols")
         bo_all = const.tile([P, D], BF16, name="bo_all")
@@ -86,7 +87,6 @@ def tile_gatedmultiscaleretentionlayer_pc_kernel(tc, x, ret, Wg, bg, Wo, bo, out
         x_tiles = {}
         ret_tiles = {}
         raw_tiles = {}
-        stat_tiles = {}
         norm_scalars = {}
         gn_tiles = {}
         gate_tiles = {}
@@ -193,51 +193,38 @@ def tile_gatedmultiscaleretentionlayer_pc_kernel(tc, x, ret, Wg, bg, Wo, bo, out
 
         def tile_statistics(i):
             q, a = divmod(i, QTILES)
-            if a == 0:
-                stat_tiles[q] = stat_pool.tile([P, HEADS, QTILES, 6], F32, name="stats")
+            stats = stat_pool.tile([P, HEADS, 6], F32, name="stats")
             for h in range(HEADS):
-                nc.vector.bn_stats(out=stat_tiles[q][:, h, a, :], in_=ret_tiles[q][:, h, a, :])
-
-        def join_statistics(q):
-            groups = HEADS * QTILES
-            by_group = stat_tiles[q][:].rearrange("p h a k -> p (h a) k")
-            mean_e, cv_e = by_group[:, :, 1], by_group[:, :, 2]
-            mean_o, cv_o = by_group[:, :, 4], by_group[:, :, 5]
-            diff = stat_pool.tile([P, groups], F32, name="diff")
-            nc.vector.tensor_tensor(out=diff[:], in0=mean_e, in1=mean_o, op=ALU.subtract)
-            mean2 = stat_pool.tile([P, groups], F32, name="mean2")
-            nc.vector.tensor_tensor(out=mean2[:], in0=mean_e, in1=mean_o, op=ALU.add)
-            diff_sq = stat_pool.tile([P, groups], F32, name="diff_sq")
-            nc.vector.tensor_tensor(out=diff_sq[:], in0=diff[:], in1=diff[:], op=ALU.mult)
-            cv = stat_pool.tile([P, groups], F32, name="cv")
-            nc.vector.tensor_tensor(out=cv[:], in0=cv_e, in1=cv_o, op=ALU.add)
-            nc.vector.scalar_tensor_tensor(
-                out=cv[:], in0=diff_sq[:], scalar=float(DV // 4), in1=cv[:], op0=ALU.mult, op1=ALU.add
-            )
-            var_eps = stat_pool.tile([P, groups], F32, name="var_eps")
-            nc.vector.tensor_scalar(
-                out=var_eps[:], in0=cv[:], scalar1=1.0 / DV, scalar2=EPS, op0=ALU.mult, op1=ALU.add
-            )
-            rstd = stat_pool.tile([P, groups], F32, name="rstd", bufs=3)
-            nc.gpsimd.tensor_tensor(out=rstd[:], in0=var_eps[:], in1=neg_half[:], op=ALU.pow)
-            shift = stat_pool.tile([P, groups], F32, name="shift", bufs=3)
-            nc.gpsimd.tensor_tensor(out=shift[:], in0=mean2[:], in1=rstd[:], op=ALU.mult)
+                nc.vector.bn_stats(out=stats[:, h, :], in_=ret_tiles[q][:, h, a, :])
+            mean_e, cv_e = stats[:, :, 1], stats[:, :, 2]
+            mean_o, cv_o = stats[:, :, 4], stats[:, :, 5]
+            diff = stat_pool.tile([P, HEADS], F32, name="diff")
+            nc.gpsimd.tensor_tensor(out=diff[:], in0=mean_e, in1=mean_o, op=ALU.subtract)
+            nc.gpsimd.tensor_tensor(out=diff[:], in0=diff[:], in1=diff[:], op=ALU.mult)
+            cv = stat_pool.tile([P, HEADS], F32, name="cv")
+            nc.gpsimd.tensor_tensor(out=cv[:], in0=cv_e, in1=cv_o, op=ALU.add)
+            nc.gpsimd.tensor_scalar(out=cv[:], in0=cv[:], scalar1=1.0 / DV, scalar2=EPS, op0=ALU.mult, op1=ALU.add)
+            nc.gpsimd.tensor_scalar(out=diff[:], in0=diff[:], scalar1=0.25, scalar2=0.0, op0=ALU.mult, op1=ALU.add)
+            nc.gpsimd.tensor_tensor(out=cv[:], in0=cv[:], in1=diff[:], op=ALU.add)
+            rstd = stat_pool.tile([P, HEADS], F32, name="rstd", bufs=STAT_LEAD + 1)
+            nc.gpsimd.tensor_tensor(out=rstd[:], in0=cv[:], in1=neg_half[:], op=ALU.pow)
+            shift = stat_pool.tile([P, HEADS], F32, name="shift", bufs=STAT_LEAD + 1)
+            nc.gpsimd.tensor_tensor(out=shift[:], in0=mean_e, in1=mean_o, op=ALU.add)
+            nc.gpsimd.tensor_tensor(out=shift[:], in0=shift[:], in1=rstd[:], op=ALU.mult)
             nc.gpsimd.tensor_scalar(out=shift[:], in0=shift[:], scalar1=-0.5, scalar2=0.0, op0=ALU.mult, op1=ALU.add)
-            norm_scalars[q] = (rstd, shift)
+            norm_scalars[i] = (rstd, shift)
 
         def normalise(i):
             q, a = divmod(i, QTILES)
-            ret_q = ret_tiles[q]
-            rstd, shift = norm_scalars[q]
+            rstd, shift = norm_scalars[i]
             gn = gn_pool.tile([P, HEADS, DV], F32, name="gn")
             for h in range(HEADS):
-                group = h * QTILES + a
                 nc.scalar.activation(
                     out=gn[:, h, :],
-                    in_=ret_q[:, h, a, :],
+                    in_=ret_tiles[q][:, h, a, :],
                     func=ACT.Identity,
-                    scale=rstd[:, group : group + 1],
-                    bias=shift[:, group : group + 1],
+                    scale=rstd[:, h : h + 1],
+                    bias=shift[:, h : h + 1],
                 )
             gn_tiles[i] = gn
 
@@ -325,7 +312,6 @@ def tile_gatedmultiscaleretentionlayer_pc_kernel(tc, x, ret, Wg, bg, Wo, bo, out
 
         tile_statistics(0)
         tile_statistics(1)
-        join_statistics(0)
         turn_bg()
         turn_x(0)
         quantise_x(0)
@@ -342,7 +328,6 @@ def tile_gatedmultiscaleretentionlayer_pc_kernel(tc, x, ret, Wg, bg, Wo, bo, out
         normalise(0)
         tile_statistics(2)
         tile_statistics(3)
-        join_statistics(1)
         for g in range(PASSES2 + 1):
             if g < PASSES2:
                 regroup_wo(g)
@@ -371,9 +356,7 @@ def tile_gatedmultiscaleretentionlayer_pc_kernel(tc, x, ret, Wg, bg, Wo, bo, out
                         gate_pair(1 + k // (HEADS // 2), k % (HEADS // 2))
                 if i + QTILES < TILES:
                     normalise(i + QTILES)
-                if i + 2 * QTILES < TILES:
-                    tile_statistics(i + 2 * QTILES)
-                    if a == 1:
-                        join_statistics(q + 2)
+                if i + STAT_LEAD < TILES:
+                    tile_statistics(i + STAT_LEAD)
                 if i + 2 < QUARTERS:
                     quantise_x(i + 2)

@@ -193,25 +193,20 @@ def tile_gatedmultiscaleretentionlayer_pc_kernel(tc, x, ret, Wg, bg, Wo, bo, out
 
         def tile_statistics(i):
             q, a = divmod(i, QTILES)
-            stats = stat_pool.tile([P, HEADS, 6], F32, name="stats")
-            for h in range(HEADS):
-                nc.vector.bn_stats(out=stats[:, h, :], in_=ret_tiles[q][:, h, a, :])
-            mean_e, cv_e = stats[:, :, 1], stats[:, :, 2]
-            mean_o, cv_o = stats[:, :, 4], stats[:, :, 5]
-            diff = stat_pool.tile([P, HEADS], F32, name="diff")
-            nc.gpsimd.tensor_tensor(out=diff[:], in0=mean_e, in1=mean_o, op=ALU.subtract)
-            nc.gpsimd.tensor_tensor(out=diff[:], in0=diff[:], in1=diff[:], op=ALU.mult)
-            cv = stat_pool.tile([P, HEADS], F32, name="cv")
-            nc.gpsimd.tensor_tensor(out=cv[:], in0=cv_e, in1=cv_o, op=ALU.add)
-            nc.gpsimd.tensor_scalar(out=cv[:], in0=cv[:], scalar1=1.0 / DV, scalar2=EPS, op0=ALU.mult, op1=ALU.add)
-            nc.gpsimd.tensor_scalar(out=diff[:], in0=diff[:], scalar1=0.25, scalar2=0.0, op0=ALU.mult, op1=ALU.add)
-            nc.gpsimd.tensor_tensor(out=cv[:], in0=cv[:], in1=diff[:], op=ALU.add)
+            stats = stat_pool.tile([P, HEADS // 2, 6], F32, name="stats")
+            for k in range(HEADS // 2):
+                nc.vector.bn_stats(
+                    out=stats[:, k, :], in_=ret_tiles[q][:, 2 * k : 2 * k + 2, a, :].rearrange("p h v -> p v h")
+                )
+            by_head = stats[:].rearrange("p k (e s) -> p (k e) s", s=3)
+            mean, cv = by_head[:, :, 1], by_head[:, :, 2]
+            var = stat_pool.tile([P, HEADS], F32, name="var")
+            nc.gpsimd.tensor_scalar(out=var[:], in0=cv, scalar1=1.0 / DV, scalar2=EPS, op0=ALU.mult, op1=ALU.add)
             rstd = stat_pool.tile([P, HEADS], F32, name="rstd", bufs=STAT_LEAD + 1)
-            nc.gpsimd.tensor_tensor(out=rstd[:], in0=cv[:], in1=neg_half[:], op=ALU.pow)
+            nc.gpsimd.tensor_tensor(out=rstd[:], in0=var[:], in1=neg_half[:], op=ALU.pow)
             shift = stat_pool.tile([P, HEADS], F32, name="shift", bufs=STAT_LEAD + 1)
-            nc.gpsimd.tensor_tensor(out=shift[:], in0=mean_e, in1=mean_o, op=ALU.add)
-            nc.gpsimd.tensor_tensor(out=shift[:], in0=shift[:], in1=rstd[:], op=ALU.mult)
-            nc.gpsimd.tensor_scalar(out=shift[:], in0=shift[:], scalar1=-0.5, scalar2=0.0, op0=ALU.mult, op1=ALU.add)
+            nc.gpsimd.tensor_tensor(out=shift[:], in0=mean, in1=rstd[:], op=ALU.mult)
+            nc.gpsimd.tensor_scalar(out=shift[:], in0=shift[:], scalar1=-1.0, scalar2=0.0, op0=ALU.mult, op1=ALU.add)
             norm_scalars[i] = (rstd, shift)
 
         def normalise(i):

@@ -29,6 +29,7 @@ PASSES2 = F // (P * PACK)
 WG_CHUNKS = 4
 WG_COLS = F // WG_CHUNKS
 N_HALF = 512
+BANK_COLS = 256
 GATE_PAIRS = 6
 OUT_LAG = 1
 STAT_LEAD = 4
@@ -179,8 +180,18 @@ def tile_gatedmultiscaleretentionlayer_pc_kernel(tc, x, ret, Wg, bg, Wo, bo, out
             wo_raw = raw_tiles["wo", g]
             wo_grouped = grp_pool.tile([P, D * PACK], BF16, name="wo_grouped", tag="w_grouped", align_bytes=64)
             grouped = wo_grouped[:].rearrange("p (n t) -> p n t", t=PACK)
-            dst, src = regroup_views(grouped[:, 0 : D // 2, :], wo_raw[:, :, 0 : D // 2])
-            nc.scalar.copy(out=dst, in_=src)
+            for b in range(D // 2 // BANK_COLS):
+                bank = ps_turn.tile([P, BANK_COLS, PACK], BF16, name="wo_bank", tag="turn")
+                for m in range(2):
+                    first = b * BANK_COLS + m * BANK_COLS // 2
+                    nc.tensor.matmul(
+                        out=bank[:, m * BANK_COLS // 2 : (m + 1) * BANK_COLS // 2, :],
+                        lhsT=ident_bf16[:],
+                        rhs=wo_raw[:, :, first : first + BANK_COLS // 2].rearrange("p t c -> p c t"),
+                        start=True,
+                        stop=True,
+                    )
+                nc.scalar.copy(out=grouped[:, b * BANK_COLS : (b + 1) * BANK_COLS, :], in_=bank[:])
             dst, src = regroup_views(grouped[:, D // 2 : D, :], wo_raw[:, :, D // 2 : D])
             nc.vector.tensor_copy(out=dst, in_=src)
             raw_tiles["wo grouped", g] = wo_grouped

@@ -28,11 +28,18 @@ PASSES1 = D // (P * PACK)
 PASSES2 = F // (P * PACK)
 WG_CHUNKS = 4
 WG_COLS = F // WG_CHUNKS
-N_HALF = 512
 BANK_COLS = 256
-GATE_PAIRS = 6
-OUT_LAG = 1
-STAT_LEAD = 4
+N_HALF = 512
+WEIGHT_CHUNKS = WG_CHUNKS + PASSES2
+UNITS = QUARTERS * PASSES2
+ITEMS = 2 * UNITS
+WEIGHT_BANKS = 24
+GATE_LAG = 3
+NORM_LAG = 4
+TURN_LAG = 6
+OUT_START = 28
+X_AT = 6
+STAT_LEAD = 2
 
 FLOPS = 2 * S * D * F + 2 * S * F * D
 
@@ -57,18 +64,19 @@ def tile_gatedmultiscaleretentionlayer_pc_kernel(tc, x, ret, Wg, bg, Wo, bo, out
         const = pools.enter_context(tc.tile_pool(name="const", bufs=1))
         codes = pools.enter_context(tc.tile_pool(name="codes", bufs=1))
         x_pool = pools.enter_context(tc.tile_pool(name="x_pool", bufs=2))
-        ret_pool = pools.enter_context(tc.tile_pool(name="ret_pool", bufs=3))
+        ret_pool = pools.enter_context(tc.tile_pool(name="ret_pool", bufs=4))
         raw_pool = pools.enter_context(tc.tile_pool(name="raw_pool", bufs=4))
         grp_pool = pools.enter_context(tc.tile_pool(name="grp_pool", bufs=2))
-        stat_pool = pools.enter_context(tc.tile_pool(name="stat_pool", bufs=2))
-        gn_pool = pools.enter_context(tc.tile_pool(name="gn_pool", bufs=2))
-        gate_pool = pools.enter_context(tc.tile_pool(name="gate_pool", bufs=3))
-        h_pool = pools.enter_context(tc.tile_pool(name="h_pool", bufs=2))
-        hc_pool = pools.enter_context(tc.tile_pool(name="hc_pool", bufs=OUT_LAG + 2))
-        out_pool = pools.enter_context(tc.tile_pool(name="out_pool", bufs=2))
+        stat_pool = pools.enter_context(tc.tile_pool(name="stat_pool", bufs=8))
+        gn_pool = pools.enter_context(tc.tile_pool(name="gn_pool", bufs=8))
+        gate_pool = pools.enter_context(tc.tile_pool(name="gate_pool", bufs=5))
+        h_pool = pools.enter_context(tc.tile_pool(name="h_pool", bufs=4))
+        hc_pool = pools.enter_context(tc.tile_pool(name="hc_pool", bufs=6))
+        out_pool = pools.enter_context(tc.tile_pool(name="out_pool", bufs=4))
         ps_gate = pools.enter_context(tc.psum_pool(name="ps_gate", bufs=3))
         ps_turn = pools.enter_context(tc.psum_pool(name="ps_turn", bufs=3))
         ps_out = pools.enter_context(tc.psum_pool(name="ps_out", bufs=2))
+        ps_w, W_TAG = ps_out, "acc"
         pools.enter_context(tc.manual_schedule())
 
         x_codes = codes.tile([P, QUARTERS * PASSES1 * QCOLS], U32, name="x_codes", align_bytes=64)
@@ -81,6 +89,7 @@ def tile_gatedmultiscaleretentionlayer_pc_kernel(tc, x, ret, Wg, bg, Wo, bo, out
         ident_f32 = const.tile([P, P], F32, name="ident_f32")
         ident_bf16 = const.tile([P, P], BF16, name="ident_bf16")
         neg_half = const.tile([P, HEADS], F32, name="neg_half")
+        zero = const.tile([P, HEADS], F32, name="zero")
         bg_rows = const.tile([P, P], BF16, name="bg_rows")
         bg_cols = const.tile([P, HEADS], F32, name="bg_cols")
         bo_all = const.tile([P, D], BF16, name="bo_all")
@@ -88,6 +97,8 @@ def tile_gatedmultiscaleretentionlayer_pc_kernel(tc, x, ret, Wg, bg, Wo, bo, out
         x_tiles = {}
         ret_tiles = {}
         raw_tiles = {}
+        grouped_tiles = {}
+        stat_tiles = {}
         norm_scalars = {}
         gn_tiles = {}
         gate_tiles = {}
@@ -99,13 +110,13 @@ def tile_gatedmultiscaleretentionlayer_pc_kernel(tc, x, ret, Wg, bg, Wo, bo, out
             nc.sync.dma_start(out=x_q[:], in_=x_rows[:, q * QTILES : (q + 1) * QTILES, :])
             x_tiles[q] = x_q
 
-        def load_ret(q):
-            ret_q = ret_pool.tile([P, HEADS, QTILES, DV], BF16, name="ret_q")
-            for heads in (slice(0, HEADS // 2), slice(HEADS // 2, HEADS)):
-                nc.sync.dma_start(
-                    out=ret_q[:, heads, :, :], in_=ret_rows[:, heads, q * QTILES : (q + 1) * QTILES, :]
-                )
-            ret_tiles[q] = ret_q
+        def load_ret(q, half):
+            if half == 0:
+                ret_tiles[q] = ret_pool.tile([P, HEADS, QTILES, DV], BF16, name="ret_q")
+            heads = slice(half * HEADS // 2, (half + 1) * HEADS // 2)
+            nc.sync.dma_start(
+                out=ret_tiles[q][:, heads, :, :], in_=ret_rows[:, heads, q * QTILES : (q + 1) * QTILES, :]
+            )
 
         def load_wg(c):
             wg_raw = raw_pool.tile([P, PASSES1 * PACK, WG_COLS], BF16, name="wg_raw", tag="raw")
@@ -133,26 +144,24 @@ def tile_gatedmultiscaleretentionlayer_pc_kernel(tc, x, ret, Wg, bg, Wo, bo, out
         def load_bo():
             nc.sync.dma_start(out=bo_all[:], in_=bo.partition_broadcast(P))
 
-        def turn_x(q):
-            x_q = x_tiles[q]
-            x_grouped = grp_pool.tile([P, PASSES1 * QCOLS * PACK], BF16, name="x_grouped", align_bytes=64)
-            grouped_words = x_grouped[:].bitcast(F32).rearrange(
+        def turn_x(q, a):
+            if a == 0:
+                x_tiles["grouped", q] = grp_pool.tile([P, PASSES1 * QCOLS * PACK], BF16, name="x_grouped", align_bytes=64)
+            grouped_words = x_tiles["grouped", q][:].bitcast(F32).rearrange(
                 "w (g c u) -> w g c u", g=PASSES1, c=QCOLS, u=2
             )
-            for a in range(QTILES):
-                words = x_q[:, a, :].bitcast(F32)
-                turned = ps_turn.tile([P, PASSES1, 2, P], F32, name="x_turned", tag="turn")
-                for g in range(PASSES1):
-                    for u in range(2):
-                        first = 256 * g + 128 * u
-                        nc.tensor.transpose(
-                            out=turned[:, g, u, :], in_=words[:, first : first + P], identity=ident_f32[:]
-                        )
-                nc.scalar.copy(
-                    out=grouped_words[:, :, a * P : (a + 1) * P, :],
-                    in_=turned[:].rearrange("w g u p -> w g p u"),
-                )
-            x_tiles["grouped", q] = x_grouped
+            words = x_tiles[q][:, a, :].bitcast(F32)
+            turned = ps_turn.tile([P, PASSES1, 2, P], F32, name="x_turned", tag="turn")
+            for g in range(PASSES1):
+                for u in range(2):
+                    first = 256 * g + 128 * u
+                    nc.tensor.transpose(
+                        out=turned[:, g, u, :], in_=words[:, first : first + P], identity=ident_f32[:]
+                    )
+            nc.scalar.copy(
+                out=grouped_words[:, :, a * P : (a + 1) * P, :],
+                in_=turned[:].rearrange("w g u p -> w g p u"),
+            )
 
         def quantise_x(q):
             cols = slice(q * PASSES1 * QCOLS, (q + 1) * PASSES1 * QCOLS)
@@ -160,103 +169,115 @@ def tile_gatedmultiscaleretentionlayer_pc_kernel(tc, x, ret, Wg, bg, Wo, bo, out
                 out=x_codes[:, cols].bitcast(FP8X4), scales=x_scales[:, cols], in_=x_tiles["grouped", q][:]
             )
 
-        def regroup_wg(c):
-            wg_raw = raw_tiles["wg", c]
-            wg_grouped = grp_pool.tile([P, PASSES1 * WG_COLS * PACK], BF16, name="wg_grouped", tag="w_grouped", align_bytes=64)
-            grouped = wg_grouped[:].rearrange("p (g f t) -> p g f t", g=PASSES1, f=WG_COLS, t=PACK)
-            dst, src = regroup_views(grouped[:, 0, :, :], wg_raw[:, 0:PACK, :])
-            nc.scalar.copy(out=dst, in_=src)
-            dst, src = regroup_views(grouped[:, 1, :, :], wg_raw[:, PACK : 2 * PACK, :])
+        def regroup_bank(grouped, raw, engine):
+            bank = ps_w.tile([P, BANK_COLS, PACK], BF16, name="w_bank", tag=W_TAG)
+            for m in range(2):
+                cols = slice(m * BANK_COLS // 2, (m + 1) * BANK_COLS // 2)
+                nc.tensor.matmul(
+                    out=bank[:, cols, :],
+                    lhsT=ident_bf16[:],
+                    rhs=raw[:, :, cols].rearrange("p t c -> p c t"),
+                    start=True,
+                    stop=True,
+                )
+            if engine == 0:
+                nc.scalar.copy(out=grouped, in_=bank[:])
+            else:
+                nc.vector.tensor_copy(out=grouped, in_=bank[:])
+
+        def wg_bank(c, b, engine):
+            if c not in grouped_tiles:
+                grouped_tiles[c] = grp_pool.tile([P, PASSES1 * WG_COLS * PACK], BF16, name="wg_grouped", tag="w_grouped", align_bytes=64)
+            grouped = grouped_tiles[c][:].rearrange("p (g f t) -> p g f t", g=PASSES1, f=WG_COLS, t=PACK)
+            cols = slice(b * BANK_COLS, (b + 1) * BANK_COLS)
+            regroup_bank(grouped[:, 0, cols, :], raw_tiles["wg", c][:, 0:PACK, cols], engine)
+
+        def wg_direct(c, b):
+            if c not in grouped_tiles:
+                grouped_tiles[c] = grp_pool.tile([P, PASSES1 * WG_COLS * PACK], BF16, name="wg_grouped", tag="w_grouped", align_bytes=64)
+            grouped = grouped_tiles[c][:].rearrange("p (g f t) -> p g f t", g=PASSES1, f=WG_COLS, t=PACK)
+            cols = slice(b * BANK_COLS, (b + 1) * BANK_COLS)
+            dst, src = regroup_views(grouped[:, 1, cols, :], raw_tiles["wg", c][:, PACK : 2 * PACK, cols])
             nc.vector.tensor_copy(out=dst, in_=src)
-            raw_tiles["wg grouped", c] = wg_grouped
+
+        def wo_bank(g, b, engine):
+            if ("wo", g) not in grouped_tiles:
+                grouped_tiles["wo", g] = grp_pool.tile([P, D * PACK], BF16, name="wo_grouped", tag="w_grouped", align_bytes=64)
+            grouped = grouped_tiles["wo", g][:].rearrange("p (n t) -> p n t", t=PACK)
+            cols = slice(b * BANK_COLS, (b + 1) * BANK_COLS)
+            regroup_bank(grouped[:, cols, :], raw_tiles["wo", g][:, :, cols], engine)
 
         def quantise_wg(c):
             cols = slice(c * PASSES1 * WG_COLS, (c + 1) * PASSES1 * WG_COLS)
             nc.vector.quantize_mx(
-                out=wg_codes[:, cols].bitcast(FP8X4), scales=wg_scales[:, cols], in_=raw_tiles["wg grouped", c][:]
+                out=wg_codes[:, cols].bitcast(FP8X4), scales=wg_scales[:, cols], in_=grouped_tiles[c][:]
             )
-
-        def regroup_wo(g):
-            wo_raw = raw_tiles["wo", g]
-            wo_grouped = grp_pool.tile([P, D * PACK], BF16, name="wo_grouped", tag="w_grouped", align_bytes=64)
-            grouped = wo_grouped[:].rearrange("p (n t) -> p n t", t=PACK)
-            for b in range(D // 2 // BANK_COLS):
-                bank = ps_turn.tile([P, BANK_COLS, PACK], BF16, name="wo_bank", tag="turn")
-                for m in range(2):
-                    first = b * BANK_COLS + m * BANK_COLS // 2
-                    nc.tensor.matmul(
-                        out=bank[:, m * BANK_COLS // 2 : (m + 1) * BANK_COLS // 2, :],
-                        lhsT=ident_bf16[:],
-                        rhs=wo_raw[:, :, first : first + BANK_COLS // 2].rearrange("p t c -> p c t"),
-                        start=True,
-                        stop=True,
-                    )
-                nc.scalar.copy(out=grouped[:, b * BANK_COLS : (b + 1) * BANK_COLS, :], in_=bank[:])
-            dst, src = regroup_views(grouped[:, D // 2 : D, :], wo_raw[:, :, D // 2 : D])
-            nc.vector.tensor_copy(out=dst, in_=src)
-            raw_tiles["wo grouped", g] = wo_grouped
 
         def quantise_wo(g):
             cols = slice(g * D, (g + 1) * D)
             nc.vector.quantize_mx(
-                out=wo_codes[:, cols].bitcast(FP8X4), scales=wo_scales[:, cols], in_=raw_tiles["wo grouped", g][:]
+                out=wo_codes[:, cols].bitcast(FP8X4), scales=wo_scales[:, cols], in_=grouped_tiles["wo", g][:]
             )
 
-        def tile_statistics(i):
+        def statistics(i, half):
             q, a = divmod(i, QTILES)
-            stats = stat_pool.tile([P, HEADS // 2, 6], F32, name="stats")
-            for k in range(HEADS // 2):
+            if half == 0:
+                stat_tiles[i] = stat_pool.tile([P, HEADS // 2, 6], F32, name="stats")
+            stats = stat_tiles[i]
+            for k in range(half * HEADS // 4, (half + 1) * HEADS // 4):
                 nc.vector.bn_stats(
                     out=stats[:, k, :], in_=ret_tiles[q][:, 2 * k : 2 * k + 2, a, :].rearrange("p h v -> p v h")
                 )
-            by_head = stats[:].rearrange("p k (e s) -> p (k e) s", s=3)
+
+        def norm_scales(i):
+            by_head = stat_tiles[i][:].rearrange("p k (e s) -> p (k e) s", s=3)
             mean, cv = by_head[:, :, 1], by_head[:, :, 2]
             var = stat_pool.tile([P, HEADS], F32, name="var")
-            nc.gpsimd.tensor_scalar(out=var[:], in0=cv, scalar1=1.0 / DV, scalar2=EPS, op0=ALU.mult, op1=ALU.add)
-            rstd = stat_pool.tile([P, HEADS], F32, name="rstd", bufs=STAT_LEAD + 1)
+            nc.vector.tensor_scalar(out=var[:], in0=cv, scalar1=1.0 / DV, scalar2=EPS, op0=ALU.mult, op1=ALU.add)
+            rstd = stat_pool.tile([P, HEADS], F32, name="rstd")
             nc.gpsimd.tensor_tensor(out=rstd[:], in0=var[:], in1=neg_half[:], op=ALU.pow)
-            shift = stat_pool.tile([P, HEADS], F32, name="shift", bufs=STAT_LEAD + 1)
+            shift = stat_pool.tile([P, HEADS], F32, name="shift")
             nc.gpsimd.tensor_tensor(out=shift[:], in0=mean, in1=rstd[:], op=ALU.mult)
-            nc.gpsimd.tensor_scalar(out=shift[:], in0=shift[:], scalar1=-1.0, scalar2=0.0, op0=ALU.mult, op1=ALU.add)
+            nc.gpsimd.tensor_tensor(out=shift[:], in0=zero[:], in1=shift[:], op=ALU.subtract)
             norm_scalars[i] = (rstd, shift)
 
-        def normalise(i):
+        def normalise(i, g):
             q, a = divmod(i, QTILES)
             rstd, shift = norm_scalars[i]
-            gn = gn_pool.tile([P, HEADS, DV], F32, name="gn")
-            for h in range(HEADS):
+            gn = gn_pool.tile([P, PACK, DV], F32, name="gn")
+            for t in range(PACK):
+                h = PACK * g + t
                 nc.scalar.activation(
-                    out=gn[:, h, :],
+                    out=gn[:, t, :],
                     in_=ret_tiles[q][:, h, a, :],
                     func=ACT.Identity,
                     scale=rstd[:, h : h + 1],
                     bias=shift[:, h : h + 1],
                 )
-            gn_tiles[i] = gn
+            gn_tiles[i, g] = gn
 
-        def gate_pair(q, pair):
+        def gate_pair(q, g, pair):
             if pair == 0:
-                gate_tiles[q] = gate_pool.tile([P, HEADS, QCOLS], F32, name="gate")
-            gate = gate_tiles[q]
+                gate_tiles[q, g] = gate_pool.tile([P, PACK, QCOLS], F32, name="gate")
             bank = ps_gate.tile([P, 2, QCOLS], F32, name="gate_bank")
             for k in range(2):
-                c, r = divmod(2 * pair + k, WG_COLS // P)
-                for g in range(PASSES1):
-                    w_cols = slice((c * PASSES1 + g) * WG_COLS + r * P, (c * PASSES1 + g) * WG_COLS + (r + 1) * P)
-                    x_cols = slice((q * PASSES1 + g) * QCOLS, (q * PASSES1 + g + 1) * QCOLS)
+                r = 2 * pair + k
+                for p in range(PASSES1):
+                    w_cols = slice((g * PASSES1 + p) * WG_COLS + r * P, (g * PASSES1 + p) * WG_COLS + (r + 1) * P)
+                    x_cols = slice((q * PASSES1 + p) * QCOLS, (q * PASSES1 + p + 1) * QCOLS)
                     nc.tensor.matmul_mx(
                         out=bank[:, k, :],
                         lhsT=wg_codes[:, w_cols].bitcast(FP8X4),
                         lhsT_scale=wg_scales[:, w_cols],
                         rhs=x_codes[:, x_cols].bitcast(FP8X4),
                         rhs_scale=x_scales[:, x_cols],
-                        start=(g == 0),
-                        stop=(g == PASSES1 - 1),
+                        start=(p == 0),
+                        stop=(p == PASSES1 - 1),
                     )
             for k in range(2):
-                head = 2 * pair + k
+                head = PACK * g + 2 * pair + k
                 nc.scalar.activation(
-                    out=gate[:, head, :],
+                    out=gate_tiles[q, g][:, 2 * pair + k, :],
                     in_=bank[:, k, :],
                     func=ACT.Silu,
                     bias=bg_cols[:, head : head + 1],
@@ -265,15 +286,15 @@ def tile_gatedmultiscaleretentionlayer_pc_kernel(tc, x, ret, Wg, bg, Wo, bo, out
 
         def turn_and_multiply(i, g):
             q, a = divmod(i, QTILES)
-            if g == 0:
+            if i not in h_tiles:
                 h_tiles[i] = h_pool.tile([P, PASSES2 * P * PACK], BF16, name="h_grouped", align_bytes=64)
             grouped = h_tiles[i][:].rearrange("v (g p t) -> v g p t", g=PASSES2, p=P, t=PACK)
             turned = ps_turn.tile([P, PACK, P], F32, name="gn_turned", tag="turn")
             for t in range(PACK):
-                nc.tensor.transpose(out=turned[:, t, :], in_=gn_tiles[i][:, PACK * g + t, :], identity=ident_f32[:])
+                nc.tensor.transpose(out=turned[:, t, :], in_=gn_tiles[i, g][:, t, :], identity=ident_f32[:])
             nc.vector.tensor_tensor(
                 out=grouped[:, g, :, :],
-                in0=gate_tiles[q][:, PACK * g : PACK * (g + 1), a * P : (a + 1) * P].rearrange("v t p -> v p t"),
+                in0=gate_tiles[q, g][:, :, a * P : (a + 1) * P].rearrange("v t p -> v p t"),
                 in1=turned[:].rearrange("v t p -> v p t"),
                 op=ALU.mult,
             )
@@ -284,85 +305,107 @@ def tile_gatedmultiscaleretentionlayer_pc_kernel(tc, x, ret, Wg, bg, Wo, bo, out
             nc.vector.quantize_mx(out=h_codes[:].bitcast(FP8X4), scales=h_scales[:], in_=h_tiles[i][:])
             hc_tiles[i] = (h_codes, h_scales)
 
-        def out_tile(i):
+        def out_half(i, half):
             h_codes, h_scales = hc_tiles[i]
-            result = out_pool.tile([P, D], F32, name="result")
-            for half in range(D // N_HALF):
-                acc = ps_out.tile([P, N_HALF], F32, name="acc")
-                for g in range(PASSES2):
-                    h_cols = slice(g * P, (g + 1) * P)
-                    n_cols = slice(g * D + half * N_HALF, g * D + (half + 1) * N_HALF)
-                    nc.tensor.matmul_mx(
-                        out=acc[:],
-                        lhsT=h_codes[:, h_cols].bitcast(FP8X4),
-                        lhsT_scale=h_scales[:, h_cols],
-                        rhs=wo_codes[:, n_cols].bitcast(FP8X4),
-                        rhs_scale=wo_scales[:, n_cols],
-                        start=(g == 0),
-                        stop=(g == PASSES2 - 1),
-                    )
-                n_out = slice(half * N_HALF, (half + 1) * N_HALF)
-                nc.vector.tensor_tensor(out=result[:, n_out], in0=acc[:], in1=bo_all[:, n_out], op=ALU.add)
-            nc.sync.dma_start(out=out_rows[:, i, :], in_=result[:])
+            result = out_pool.tile([P, N_HALF], F32, name="result")
+            acc = ps_out.tile([P, N_HALF], F32, name="acc")
+            for g in range(PASSES2):
+                h_cols = slice(g * P, (g + 1) * P)
+                n_cols = slice(g * D + half * N_HALF, g * D + (half + 1) * N_HALF)
+                nc.tensor.matmul_mx(
+                    out=acc[:],
+                    lhsT=h_codes[:, h_cols].bitcast(FP8X4),
+                    lhsT_scale=h_scales[:, h_cols],
+                    rhs=wo_codes[:, n_cols].bitcast(FP8X4),
+                    rhs_scale=wo_scales[:, n_cols],
+                    start=(g == 0),
+                    stop=(g == PASSES2 - 1),
+                )
+            n_out = slice(half * N_HALF, (half + 1) * N_HALF)
+            nc.vector.tensor_tensor(out=result[:], in0=acc[:], in1=bo_all[:, n_out], op=ALU.add)
+            nc.sync.dma_start(out=out_rows[:, i, n_out], in_=result[:])
 
         make_identity(nc, ident_f32[:])
         make_identity(nc, ident_bf16[:])
         nc.vector.memset(neg_half[:], -0.5)
+        nc.vector.memset(zero[:], 0.0)
         load_bg()
-        load_ret(0)
+        load_ret(0, 0)
         load_x(0)
+        load_ret(0, 1)
         for c in range(WG_CHUNKS):
             load_wg(c)
-        load_ret(1)
         load_x(1)
+        load_ret(1, 0)
+        load_ret(1, 1)
 
-        tile_statistics(0)
-        tile_statistics(1)
+        statistics(0, 0)
+        statistics(1, 0)
+        turn_x(0, 0)
+        turn_x(0, 1)
+        statistics(0, 1)
+        norm_scales(0)
+        statistics(1, 1)
+        norm_scales(1)
         turn_bg()
-        turn_x(0)
         quantise_x(0)
-        for c in range(WG_CHUNKS + 1):
-            if c < WG_CHUNKS:
-                regroup_wg(c)
-                load_wo(c)
-            if c >= 1:
-                quantise_wg(c - 1)
-                gate_pair(0, 2 * (c - 1))
-                gate_pair(0, 2 * (c - 1) + 1)
-        load_x(2)
-        load_ret(2)
-        normalise(0)
-        tile_statistics(2)
-        tile_statistics(3)
-        for g in range(PASSES2 + 1):
-            if g < PASSES2:
-                regroup_wo(g)
-            if g >= 1:
-                quantise_wo(g - 1)
-        turn_x(1)
-        load_x(3)
-        normalise(1)
-        load_ret(3)
-        load_bo()
-        quantise_x(1)
-
-        for i in range(TILES + OUT_LAG):
-            q, a = divmod(i, QTILES)
-            if i < TILES:
-                for g in range(PASSES2):
-                    turn_and_multiply(i, g)
-                if i + 2 < QUARTERS:
-                    turn_x(i + 2)
-                quantise_h(i)
-            if i >= OUT_LAG:
-                out_tile(i - OUT_LAG)
-            if i < TILES:
-                for k in range(GATE_PAIRS * i, GATE_PAIRS * (i + 1)):
-                    if k < (QUARTERS - 1) * HEADS // 2:
-                        gate_pair(1 + k // (HEADS // 2), k % (HEADS // 2))
-                if i + QTILES < TILES:
-                    normalise(i + QTILES)
-                if i + STAT_LEAD < TILES:
-                    tile_statistics(i + STAT_LEAD)
-                if i + 2 < QUARTERS:
-                    quantise_x(i + 2)
+        quantised = 0
+        outs = [(i, half) for i in range(TILES) for half in range(2)]
+        for s in range(ITEMS + TURN_LAG + 1):
+            if s < 2 * WG_CHUNKS:
+                c, b = divmod(s, 2)
+                wg_bank(c, b, 0)
+                wg_direct(c, b)
+                if b == 1:
+                    load_wo(c)
+                    if c == 0:
+                        load_bo()
+            elif s < WEIGHT_BANKS:
+                g, b = divmod(s - 2 * WG_CHUNKS, 4)
+                wo_bank(g, b, 1 if b >= 4 - 1 else 0)
+            if s == 2 * WG_CHUNKS - 1:
+                for q in range(2, QUARTERS):
+                    load_x(q)
+                    load_ret(q, 0)
+                    load_ret(q, 1)
+            k = s - 2
+            if 0 <= k < 2 * WG_CHUNKS and k % 2 == 0:
+                quantise_wg(k // 2)
+            k = s - 2 * WG_CHUNKS - 4
+            if k >= 0 and k % 4 == 0 and k < 16:
+                quantise_wo(k // 4)
+            k = s - TURN_LAG
+            if 0 <= k < ITEMS:
+                q, r = divmod(k, 2 * PASSES2)
+                turn_and_multiply(QTILES * q + r % 2, r // 2)
+            k = s - NORM_LAG
+            if 0 <= k < ITEMS:
+                q, r = divmod(k, 2 * PASSES2)
+                normalise(QTILES * q + r % 2, r // 2)
+            if s >= OUT_START and outs and quantised > outs[0][0]:
+                out_half(*outs[0])
+                outs = outs[1:]
+            q, k = divmod(s - X_AT, 8)
+            if k < 2 and 0 <= q < QUARTERS - 1:
+                turn_x(q + 1, k)
+            k = s - GATE_LAG
+            if 0 <= k < ITEMS:
+                q, r = divmod(k, 2 * PASSES2)
+                gate_pair(q, r // 2, r % 2)
+            q, k = divmod(s + STAT_LEAD, 8)
+            if k < 4 and 1 <= q < QUARTERS:
+                i, half = divmod(2 * QTILES * q + k, 2)
+                statistics(i, half)
+                if half == 1:
+                    norm_scales(i)
+            q, k = divmod(s - X_AT - 2, 8)
+            if k == 0 and 0 <= q < QUARTERS - 1:
+                quantise_x(q + 1)
+            k = s - TURN_LAG - 1
+            if k >= 0 and k % 8 in (6, 7):
+                quantise_h(QTILES * (k // 8) + k % 8 - 6)
+                quantised += 1
+        if quantised < TILES:
+            quantise_h(TILES - 1)
+        for i, half in outs:
+            out_half(i, half)

@@ -213,6 +213,17 @@ def tile_gatedmultiscaleretentionlayer_pc_kernel(tc, x, ret, Wg, bg, Wo, bo, out
                 out=wg_codes[:, cols].bitcast(FP8X4), scales=wg_scales[:, cols], in_=grouped_tiles[c][:]
             )
 
+        def wo_direct(g, b, vector):
+            if ("wo", g) not in grouped_tiles:
+                grouped_tiles["wo", g] = grp_pool.tile([P, D * PACK], BF16, name="wo_grouped", tag="w_grouped", align_bytes=64)
+            grouped = grouped_tiles["wo", g][:].rearrange("p (n t) -> p n t", t=PACK)
+            cols = slice(b * BANK_COLS, (b + 1) * BANK_COLS)
+            dst, src = regroup_views(grouped[:, cols, :], raw_tiles["wo", g][:, :, cols])
+            if vector:
+                nc.vector.tensor_copy(out=dst, in_=src)
+            else:
+                nc.scalar.copy(out=dst, in_=src)
+
         def quantise_wo(g):
             cols = slice(g * D, (g + 1) * D)
             nc.vector.quantize_mx(
@@ -351,7 +362,13 @@ def tile_gatedmultiscaleretentionlayer_pc_kernel(tc, x, ret, Wg, bg, Wo, bo, out
         quantise_x(0)
         quantised = 0
         outs = [(i, half) for i in range(TILES) for half in range(2)]
-        for s in range(ITEMS + TURN_LAG + 1):
+        done = []
+
+        def item(k):
+            q, r = divmod(k, 2 * PASSES2)
+            return QTILES * q + r % 2, r // 2
+
+        def step_weights(s):
             if s < 2 * WG_CHUNKS:
                 c, b = divmod(s, 2)
                 wg_bank(c, b, 0)
@@ -362,50 +379,80 @@ def tile_gatedmultiscaleretentionlayer_pc_kernel(tc, x, ret, Wg, bg, Wo, bo, out
                         load_bo()
             elif s < WEIGHT_BANKS:
                 g, b = divmod(s - 2 * WG_CHUNKS, 4)
-                wo_bank(g, b, 1 if b >= 4 - 1 else 0)
+                way = "sSsV"[b]
+                if way in "SV":
+                    wo_direct(g, b, way == "V")
+                else:
+                    wo_bank(g, b, 1 if way == "v" else 0)
             if s == 2 * WG_CHUNKS - 1:
                 for q in range(2, QUARTERS):
                     load_x(q)
                     load_ret(q, 0)
                     load_ret(q, 1)
+
+        def step_quantise_weights(s):
             k = s - 2
             if 0 <= k < 2 * WG_CHUNKS and k % 2 == 0:
                 quantise_wg(k // 2)
-            k = s - 2 * WG_CHUNKS - 4
+            k = s - 2 * WG_CHUNKS - 5
             if k >= 0 and k % 4 == 0 and k < 16:
                 quantise_wo(k // 4)
+
+        def step_product(s):
             k = s - TURN_LAG
             if 0 <= k < ITEMS:
-                q, r = divmod(k, 2 * PASSES2)
-                turn_and_multiply(QTILES * q + r % 2, r // 2)
+                turn_and_multiply(*item(k))
+
+        def step_normalise(s):
             k = s - NORM_LAG
             if 0 <= k < ITEMS:
-                q, r = divmod(k, 2 * PASSES2)
-                normalise(QTILES * q + r % 2, r // 2)
-            if s >= OUT_START and outs and quantised > outs[0][0]:
+                normalise(*item(k))
+
+        def step_out(s):
+            if s >= OUT_START and outs and outs[0][0] in done:
                 out_half(*outs[0])
-                outs = outs[1:]
+                outs.remove(outs[0])
+
+        def step_turn_x(s):
             q, k = divmod(s - X_AT, 8)
             if k < 2 and 0 <= q < QUARTERS - 1:
                 turn_x(q + 1, k)
-            k = s - GATE_LAG
-            if 0 <= k < ITEMS:
-                q, r = divmod(k, 2 * PASSES2)
-                gate_pair(q, r // 2, r % 2)
+
+        def step_gate(s):
+            ks = [s - GATE_LAG]
+            for k in ks:
+                if 0 <= k < ITEMS:
+                    q, r = divmod(k, 2 * PASSES2)
+                    gate_pair(q, r // 2, r % 2)
+
+        def step_statistics(s):
             q, k = divmod(s + STAT_LEAD, 8)
             if k < 4 and 1 <= q < QUARTERS:
                 i, half = divmod(2 * QTILES * q + k, 2)
                 statistics(i, half)
                 if half == 1:
                     norm_scales(i)
+
+        def step_quantise_x(s):
             q, k = divmod(s - X_AT - 2, 8)
             if k == 0 and 0 <= q < QUARTERS - 1:
                 quantise_x(q + 1)
+
+        def step_quantise_h(s):
             k = s - TURN_LAG - 1
-            if k >= 0 and k % 8 in (6, 7):
-                quantise_h(QTILES * (k // 8) + k % 8 - 6)
-                quantised += 1
-        if quantised < TILES:
-            quantise_h(TILES - 1)
+            if 0 <= k < ITEMS and item(k)[1] == PASSES2 - 1:
+                quantise_h(item(k)[0])
+                done.append(item(k)[0])
+
+        for s in range(ITEMS + TURN_LAG + 1):
+            step_weights(s)
+            step_quantise_weights(s)
+            if s % 2 == 0:
+                step_product(s);step_normalise(s);step_out(s);step_turn_x(s);step_gate(s)
+            else:
+                step_gate(s);step_normalise(s);step_out(s);step_turn_x(s);step_product(s)
+            step_statistics(s)
+            step_quantise_x(s)
+            step_quantise_h(s)
         for i, half in outs:
             out_half(i, half)

@@ -304,9 +304,9 @@ def tile_gatedmultiscaleretentionlayer_pc_kernel(tc, x, ret, Wg, bg, Wo, bo, out
             for t in range(PACK):
                 nc.tensor.transpose(out=turned[:, t, :], in_=gn_tiles[i, g][:, t, :], identity=ident_f32[:])
             nc.vector.tensor_tensor(
-                out=grouped[:, g, :, :],
-                in0=gate_tiles[q, g][:, :, a * P : (a + 1) * P].rearrange("v t p -> v p t"),
-                in1=turned[:].rearrange("v t p -> v p t"),
+                out=grouped[:, g, :, :].rearrange("v (c i) t -> v c t i", i=4),
+                in0=gate_tiles[q, g][:, :, a * P : (a + 1) * P].rearrange("v t (c i) -> v c t i", i=4),
+                in1=turned[:].rearrange("v t (c i) -> v c t i", i=4),
                 op=ALU.mult,
             )
 

from contextlib import ExitStack

import concourse.mybir as mybir
from concourse.masks import make_identity

F32 = mybir.dt.float32
BF16 = mybir.dt.bfloat16
U32 = mybir.dt.uint32
U8 = mybir.dt.uint8
FP8X4 = mybir.dt.float8_e4m3fn_x4
ALU = mybir.AluOpType
ACT = mybir.ActivationFunctionType

P = 128
PACK = 4
S = 1024
D = 1024
HEADS = 16
DV = 128
F = HEADS * DV
EPS = 1e-5

TILES = S // P
QUARTERS = 4
QCOLS = S // QUARTERS
QTILES = TILES // QUARTERS
PASSES1 = D // (P * PACK)
PASSES2 = F // (P * PACK)
WG_CHUNKS = 4
WG_COLS = F // WG_CHUNKS
BANK_COLS = 256
N_HALF = 512
WEIGHT_CHUNKS = WG_CHUNKS + PASSES2
UNITS = QUARTERS * PASSES2
ITEMS = 2 * UNITS
WEIGHT_BANKS = 24
GATE_LAG = 3
NORM_LAG = 4
TURN_LAG = 6
OUT_START = 28
X_AT = 6
STAT_LEAD = 2

FLOPS = 2 * S * D * F + 2 * S * F * D


def regroup_views(dst, src):
    return (
        dst.rearrange("p (c i) t -> p c t i", i=4),
        src.rearrange("p t (c i) -> p c t i", i=4),
    )


def tile_gatedmultiscaleretentionlayer_pc_kernel(tc, x, ret, Wg, bg, Wo, bo, out):
    nc = tc.nc

    x_rows = x.flatten_outer_dims().rearrange("(p i) d -> p i d", i=TILES)
    ret_rows = ret.rearrange("b h (p i) v -> p (b h) i v", i=TILES)
    wg_rows = Wg.rearrange("(a p e) f -> p a e f", a=2 * PASSES1, p=P, e=2)
    wo_rows = Wo.rearrange("(g t p) n -> p g t n", g=PASSES2, t=PACK, p=P)
    out_rows = out.flatten_outer_dims().rearrange("(p i) n -> p i n", i=TILES)

    with ExitStack() as pools:
        const = pools.enter_context(tc.tile_pool(name="const", bufs=1))
        codes = pools.enter_context(tc.tile_pool(name="codes", bufs=1))
        x_pool = pools.enter_context(tc.tile_pool(name="x_pool", bufs=2))
        ret_pool = pools.enter_context(tc.tile_pool(name="ret_pool", bufs=4))
        raw_pool = pools.enter_context(tc.tile_pool(name="raw_pool", bufs=4))
        grp_pool = pools.enter_context(tc.tile_pool(name="grp_pool", bufs=2))
        stat_pool = pools.enter_context(tc.tile_pool(name="stat_pool", bufs=8))
        gn_pool = pools.enter_context(tc.tile_pool(name="gn_pool", bufs=8))
        gate_pool = pools.enter_context(tc.tile_pool(name="gate_pool", bufs=5))
        h_pool = pools.enter_context(tc.tile_pool(name="h_pool", bufs=4))
        hc_pool = pools.enter_context(tc.tile_pool(name="hc_pool", bufs=6))
        out_pool = pools.enter_context(tc.tile_pool(name="out_pool", bufs=4))
        ps_gate = pools.enter_context(tc.psum_pool(name="ps_gate", bufs=3))
        ps_turn = pools.enter_context(tc.psum_pool(name="ps_turn", bufs=3))
        ps_out = pools.enter_context(tc.psum_pool(name="ps_out", bufs=2))
        ps_w, W_TAG = ps_out, "acc"
        pools.enter_context(tc.manual_schedule())

        x_codes = codes.tile([P, QUARTERS * PASSES1 * QCOLS], U32, name="x_codes", align_bytes=64)
        x_scales = codes.tile([P, QUARTERS * PASSES1 * QCOLS], U8, name="x_scales", align_bytes=64)
        wg_codes = codes.tile([P, WG_CHUNKS * PASSES1 * WG_COLS], U32, name="wg_codes", align_bytes=64)
        wg_scales = codes.tile([P, WG_CHUNKS * PASSES1 * WG_COLS], U8, name="wg_scales", align_bytes=64)
        wo_codes = codes.tile([P, PASSES2 * D], U32, name="wo_codes", align_bytes=64)
        wo_scales = codes.tile([P, PASSES2 * D], U8, name="wo_scales", align_bytes=64)

        ident_f32 = const.tile([P, P], F32, name="ident_f32")
        ident_bf16 = const.tile([P, P], BF16, name="ident_bf16")
        neg_half = const.tile([P, HEADS], F32, name="neg_half")
        zero = const.tile([P, HEADS], F32, name="zero")
        bg_rows = const.tile([P, P], BF16, name="bg_rows")
        bg_cols = const.tile([P, HEADS], F32, name="bg_cols")
        bo_all = const.tile([P, D], BF16, name="bo_all")

        x_tiles = {}
        ret_tiles = {}
        raw_tiles = {}
        grouped_tiles = {}
        stat_tiles = {}
        norm_scalars = {}
        gn_tiles = {}
        gate_tiles = {}
        h_tiles = {}
        hc_tiles = {}

        def load_x(q):
            x_q = x_pool.tile([P, QTILES, D], BF16, name="x_q")
            nc.sync.dma_start(out=x_q[:], in_=x_rows[:, q * QTILES : (q + 1) * QTILES, :])
            x_tiles[q] = x_q

        def load_ret(q, half):
            if half == 0:
                ret_tiles[q] = ret_pool.tile([P, HEADS, QTILES, DV], BF16, name="ret_q")
            heads = slice(half * HEADS // 2, (half + 1) * HEADS // 2)
            nc.sync.dma_start(
                out=ret_tiles[q][:, heads, :, :], in_=ret_rows[:, heads, q * QTILES : (q + 1) * QTILES, :]
            )

        def load_wg(c):
            wg_raw = raw_pool.tile([P, PASSES1 * PACK, WG_COLS], BF16, name="wg_raw", tag="raw")
            by_e = wg_raw[:].rearrange("p (a e) f -> p a e f", e=2)
            for e in range(2):
                nc.sync.dma_start(
                    out=by_e[:, :, e, :], in_=wg_rows[:, :, e, c * WG_COLS : (c + 1) * WG_COLS]
                )
            raw_tiles["wg", c] = wg_raw

        def load_wo(g):
            wo_raw = raw_pool.tile([P, PACK, D], BF16, name="wo_raw", tag="raw")
            nc.sync.dma_start(out=wo_raw[:], in_=wo_rows[:, g, :, :])
            raw_tiles["wo", g] = wo_raw

        def load_bg():
            nc.vector.memset(bg_rows[:], 0.0)
            nc.sync.dma_start(out=bg_rows[0:HEADS, :], in_=bg.rearrange("(j p) -> j p", p=P))

        def turn_bg():
            bg_turned = ps_turn.tile([P, P], BF16, name="bg_turned", tag="turn")
            nc.tensor.transpose(out=bg_turned[:], in_=bg_rows[:], identity=ident_bf16[:])
            nc.vector.tensor_copy(out=bg_cols[:], in_=bg_turned[:, 0:HEADS])

        def load_bo():
            nc.sync.dma_start(out=bo_all[:], in_=bo.partition_broadcast(P))

        def turn_x(q, a):
            if a == 0:
                x_tiles["grouped", q] = grp_pool.tile([P, PASSES1 * QCOLS * PACK], BF16, name="x_grouped", align_bytes=64)
            grouped_words = x_tiles["grouped", q][:].bitcast(F32).rearrange(
                "w (g c u) -> w g c u", g=PASSES1, c=QCOLS, u=2
            )
            words = x_tiles[q][:, a, :].bitcast(F32)
            turned = ps_turn.tile([P, PASSES1, 2, P], F32, name="x_turned", tag="turn")
            for g in range(PASSES1):
                for u in range(2):
                    first = 256 * g + 128 * u
                    nc.tensor.transpose(
                        out=turned[:, g, u, :], in_=words[:, first : first + P], identity=ident_f32[:]
                    )
            nc.scalar.copy(
                out=grouped_words[:, :, a * P : (a + 1) * P, :],
                in_=turned[:].rearrange("w g u p -> w g p u"),
            )

        def quantise_x(q):
            cols = slice(q * PASSES1 * QCOLS, (q + 1) * PASSES1 * QCOLS)
            nc.vector.quantize_mx(
                out=x_codes[:, cols].bitcast(FP8X4), scales=x_scales[:, cols], in_=x_tiles["grouped", q][:]
            )

        def regroup_bank(grouped, raw, engine):
            bank = ps_w.tile([P, BANK_COLS, PACK], BF16, name="w_bank", tag=W_TAG)
            for m in range(2):
                cols = slice(m * BANK_COLS // 2, (m + 1) * BANK_COLS // 2)
                nc.tensor.matmul(
                    out=bank[:, cols, :],
                    lhsT=ident_bf16[:],
                    rhs=raw[:, :, cols].rearrange("p t c -> p c t"),
                    start=True,
                    stop=True,
                )
            if engine == 0:
                nc.scalar.copy(out=grouped, in_=bank[:])
            else:
                nc.vector.tensor_copy(out=grouped, in_=bank[:])

        def wg_bank(c, b, engine):
            if c not in grouped_tiles:
                grouped_tiles[c] = grp_pool.tile([P, PASSES1 * WG_COLS * PACK], BF16, name="wg_grouped", tag="w_grouped", align_bytes=64)
            grouped = grouped_tiles[c][:].rearrange("p (g f t) -> p g f t", g=PASSES1, f=WG_COLS, t=PACK)
            cols = slice(b * BANK_COLS, (b + 1) * BANK_COLS)
            regroup_bank(grouped[:, 0, cols, :], raw_tiles["wg", c][:, 0:PACK, cols], engine)

        def wg_direct(c, b):
            if c not in grouped_tiles:
                grouped_tiles[c] = grp_pool.tile([P, PASSES1 * WG_COLS * PACK], BF16, name="wg_grouped", tag="w_grouped", align_bytes=64)
            grouped = grouped_tiles[c][:].rearrange("p (g f t) -> p g f t", g=PASSES1, f=WG_COLS, t=PACK)
            cols = slice(b * BANK_COLS, (b + 1) * BANK_COLS)
            dst, src = regroup_views(grouped[:, 1, cols, :], raw_tiles["wg", c][:, PACK : 2 * PACK, cols])
            nc.vector.tensor_copy(out=dst, in_=src)

        def wo_bank(g, b, engine):
            if ("wo", g) not in grouped_tiles:
                grouped_tiles["wo", g] = grp_pool.tile([P, D * PACK], BF16, name="wo_grouped", tag="w_grouped", align_bytes=64)
            grouped = grouped_tiles["wo", g][:].rearrange("p (n t) -> p n t", t=PACK)
            cols = slice(b * BANK_COLS, (b + 1) * BANK_COLS)
            regroup_bank(grouped[:, cols, :], raw_tiles["wo", g][:, :, cols], engine)

        def quantise_wg(c):
            cols = slice(c * PASSES1 * WG_COLS, (c + 1) * PASSES1 * WG_COLS)
            nc.vector.quantize_mx(
                out=wg_codes[:, cols].bitcast(FP8X4), scales=wg_scales[:, cols], in_=grouped_tiles[c][:]
            )

        def wo_direct(g, b, vector):
            if ("wo", g) not in grouped_tiles:
                grouped_tiles["wo", g] = grp_pool.tile([P, D * PACK], BF16, name="wo_grouped", tag="w_grouped", align_bytes=64)
            grouped = grouped_tiles["wo", g][:].rearrange("p (n t) -> p n t", t=PACK)
            cols = slice(b * BANK_COLS, (b + 1) * BANK_COLS)
            dst, src = regroup_views(grouped[:, cols, :], raw_tiles["wo", g][:, :, cols])
            if vector:
                nc.vector.tensor_copy(out=dst, in_=src)
            else:
                nc.scalar.copy(out=dst, in_=src)

        def quantise_wo(g):
            cols = slice(g * D, (g + 1) * D)
            nc.vector.quantize_mx(
                out=wo_codes[:, cols].bitcast(FP8X4), scales=wo_scales[:, cols], in_=grouped_tiles["wo", g][:]
            )

        def statistics(i, half):
            q, a = divmod(i, QTILES)
            if half == 0:
                stat_tiles[i] = stat_pool.tile([P, HEADS // 2, 6], F32, name="stats")
            stats = stat_tiles[i]
            for k in range(half * HEADS // 4, (half + 1) * HEADS // 4):
                nc.vector.bn_stats(
                    out=stats[:, k, :], in_=ret_tiles[q][:, 2 * k : 2 * k + 2, a, :].rearrange("p h v -> p v h")
                )

        def norm_scales(i):
            by_head = stat_tiles[i][:].rearrange("p k (e s) -> p (k e) s", s=3)
            mean, cv = by_head[:, :, 1], by_head[:, :, 2]
            var = stat_pool.tile([P, HEADS], F32, name="var")
            nc.vector.tensor_scalar(out=var[:], in0=cv, scalar1=1.0 / DV, scalar2=EPS, op0=ALU.mult, op1=ALU.add)
            rstd = stat_pool.tile([P, HEADS], F32, name="rstd")
            nc.gpsimd.tensor_tensor(out=rstd[:], in0=var[:], in1=neg_half[:], op=ALU.pow)
            shift = stat_pool.tile([P, HEADS], F32, name="shift")
            nc.gpsimd.tensor_tensor(out=shift[:], in0=mean, in1=rstd[:], op=ALU.mult)
            nc.gpsimd.tensor_tensor(out=shift[:], in0=zero[:], in1=shift[:], op=ALU.subtract)
            norm_scalars[i] = (rstd, shift)

        def normalise(i, g):
            q, a = divmod(i, QTILES)
            rstd, shift = norm_scalars[i]
            gn = gn_pool.tile([P, PACK, DV], F32, name="gn")
            for t in range(PACK):
                h = PACK * g + t
                nc.scalar.activation(
                    out=gn[:, t, :],
                    in_=ret_tiles[q][:, h, a, :],
                    func=ACT.Identity,
                    scale=rstd[:, h : h + 1],
                    bias=shift[:, h : h + 1],
                )
            gn_tiles[i, g] = gn

        def gate_pair(q, g, pair):
            if pair == 0:
                gate_tiles[q, g] = gate_pool.tile([P, PACK, QCOLS], F32, name="gate")
            bank = ps_gate.tile([P, 2, QCOLS], F32, name="gate_bank")
            for k in range(2):
                r = 2 * pair + k
                for p in range(PASSES1):
                    w_cols = slice((g * PASSES1 + p) * WG_COLS + r * P, (g * PASSES1 + p) * WG_COLS + (r + 1) * P)
                    x_cols = slice((q * PASSES1 + p) * QCOLS, (q * PASSES1 + p + 1) * QCOLS)
                    nc.tensor.matmul_mx(
                        out=bank[:, k, :],
                        lhsT=wg_codes[:, w_cols].bitcast(FP8X4),
                        lhsT_scale=wg_scales[:, w_cols],
                        rhs=x_codes[:, x_cols].bitcast(FP8X4),
                        rhs_scale=x_scales[:, x_cols],
                        start=(p == 0),
                        stop=(p == PASSES1 - 1),
                    )
            for k in range(2):
                head = PACK * g + 2 * pair + k
                nc.scalar.activation(
                    out=gate_tiles[q, g][:, 2 * pair + k, :],
                    in_=bank[:, k, :],
                    func=ACT.Silu,
                    bias=bg_cols[:, head : head + 1],
                    scale=1.0,
                )

        def turn_and_multiply(i, g):
            q, a = divmod(i, QTILES)
            if i not in h_tiles:
                h_tiles[i] = h_pool.tile([P, PASSES2 * P * PACK], BF16, name="h_grouped", align_bytes=64)
            grouped = h_tiles[i][:].rearrange("v (g p t) -> v g p t", g=PASSES2, p=P, t=PACK)
            turned = ps_turn.tile([P, PACK, P], F32, name="gn_turned", tag="turn")
            for t in range(PACK):
                nc.tensor.transpose(out=turned[:, t, :], in_=gn_tiles[i, g][:, t, :], identity=ident_f32[:])
            nc.vector.tensor_tensor(
                out=grouped[:, g, :, :].rearrange("v (c i) t -> v c t i", i=4),
                in0=gate_tiles[q, g][:, :, a * P : (a + 1) * P].rearrange("v t (c i) -> v c t i", i=4),
                in1=turned[:].rearrange("v t (c i) -> v c t i", i=4),
                op=ALU.mult,
            )

        def quantise_h(i):
            h_codes = hc_pool.tile([P, PASSES2 * P], U32, name="h_codes", align_bytes=64)
            h_scales = hc_pool.tile([P, PASSES2 * P], U8, name="h_scales", align_bytes=64)
            nc.vector.quantize_mx(out=h_codes[:].bitcast(FP8X4), scales=h_scales[:], in_=h_tiles[i][:])
            hc_tiles[i] = (h_codes, h_scales)

        def out_half(i, half):
            h_codes, h_scales = hc_tiles[i]
            result = out_pool.tile([P, N_HALF], F32, name="result")
            acc = ps_out.tile([P, N_HALF], F32, name="acc")
            for g in range(PASSES2):
                h_cols = slice(g * P, (g + 1) * P)
                n_cols = slice(g * D + half * N_HALF, g * D + (half + 1) * N_HALF)
                nc.tensor.matmul_mx(
                    out=acc[:],
                    lhsT=h_codes[:, h_cols].bitcast(FP8X4),
                    lhsT_scale=h_scales[:, h_cols],
                    rhs=wo_codes[:, n_cols].bitcast(FP8X4),
                    rhs_scale=wo_scales[:, n_cols],
                    start=(g == 0),
                    stop=(g == PASSES2 - 1),
                )
            n_out = slice(half * N_HALF, (half + 1) * N_HALF)
            nc.vector.tensor_tensor(out=result[:], in0=acc[:], in1=bo_all[:, n_out], op=ALU.add)
            nc.sync.dma_start(out=out_rows[:, i, n_out], in_=result[:])

        make_identity(nc, ident_f32[:])
        make_identity(nc, ident_bf16[:])
        nc.vector.memset(neg_half[:], -0.5)
        nc.vector.memset(zero[:], 0.0)
        load_bg()
        load_ret(0, 0)
        load_x(0)
        load_ret(0, 1)
        for c in range(WG_CHUNKS):
            load_wg(c)
        load_x(1)
        load_ret(1, 0)
        load_ret(1, 1)

        statistics(0, 0)
        statistics(1, 0)
        turn_x(0, 0)
        turn_x(0, 1)
        statistics(0, 1)
        norm_scales(0)
        statistics(1, 1)
        norm_scales(1)
        turn_bg()
        quantise_x(0)
        quantised = 0
        outs = [(i, half) for i in range(TILES) for half in range(2)]
        done = []

        def item(k):
            q, r = divmod(k, 2 * PASSES2)
            return QTILES * q + r % 2, r // 2

        def step_weights(s):
            if s < 2 * WG_CHUNKS:
                c, b = divmod(s, 2)
                wg_bank(c, b, 0)
                wg_direct(c, b)
                if b == 1:
                    load_wo(c)
                    if c == 0:
                        load_bo()
            elif s < WEIGHT_BANKS:
                g, b = divmod(s - 2 * WG_CHUNKS, 4)
                way = "sSsV"[b]
                if way in "SV":
                    wo_direct(g, b, way == "V")
                else:
                    wo_bank(g, b, 1 if way == "v" else 0)
            if s == 2 * WG_CHUNKS - 1:
                for q in range(2, QUARTERS):
                    load_x(q)
                    load_ret(q, 0)
                    load_ret(q, 1)

        def step_quantise_weights(s):
            k = s - 2
            if 0 <= k < 2 * WG_CHUNKS and k % 2 == 0:
                quantise_wg(k // 2)
            k = s - 2 * WG_CHUNKS - 5
            if k >= 0 and k % 4 == 0 and k < 16:
                quantise_wo(k // 4)

        def step_product(s):
            k = s - TURN_LAG
            if 0 <= k < ITEMS:
                turn_and_multiply(*item(k))

        def step_normalise(s):
            k = s - NORM_LAG
            if 0 <= k < ITEMS:
                normalise(*item(k))

        def step_out(s):
            if s >= OUT_START and outs and outs[0][0] in done:
                out_half(*outs[0])
                outs.remove(outs[0])

        def step_turn_x(s):
            q, k = divmod(s - X_AT, 8)
            if k < 2 and 0 <= q < QUARTERS - 1:
                turn_x(q + 1, k)

        def step_gate(s):
            ks = [s - GATE_LAG]
            for k in ks:
                if 0 <= k < ITEMS:
                    q, r = divmod(k, 2 * PASSES2)
                    gate_pair(q, r // 2, r % 2)

        def step_statistics(s):
            q, k = divmod(s + STAT_LEAD, 8)
            if k < 4 and 1 <= q < QUARTERS:
                i, half = divmod(2 * QTILES * q + k, 2)
                statistics(i, half)
                if half == 1:
                    norm_scales(i)

        def step_quantise_x(s):
            q, k = divmod(s - X_AT - 2, 8)
            if k == 0 and 0 <= q < QUARTERS - 1:
                quantise_x(q + 1)

        def step_quantise_h(s):
            k = s - TURN_LAG - 1
            if 0 <= k < ITEMS and item(k)[1] == PASSES2 - 1:
                quantise_h(item(k)[0])
                done.append(item(k)[0])

        for s in range(ITEMS + TURN_LAG + 1):
            step_weights(s)
            step_quantise_weights(s)
            if s % 2 == 0:
                step_product(s);step_normalise(s);step_out(s);step_turn_x(s);step_gate(s)
            else:
                step_gate(s);step_normalise(s);step_out(s);step_turn_x(s);step_product(s)
            step_statistics(s)
            step_quantise_x(s)
            step_quantise_h(s)
        for i, half in outs:
            out_half(i, half)
